import numpy as np
import ml_dtypes


def mxq(x, axis, fmt="e4m3"):
    dtype, down = {"e4m3": (ml_dtypes.float8_e4m3fn, 7), "e5m2": (ml_dtypes.float8_e5m2, 14)}[fmt]
    v = np.moveaxis(np.asarray(x, np.float32).astype(ml_dtypes.bfloat16).astype(np.float64), axis, -1)
    blocks = v.reshape(v.shape[:-1] + (-1, 32))
    amax = np.abs(blocks).max(-1, keepdims=True)
    byte = np.maximum(np.where(amax > 0, np.frexp(amax)[1] - 1 + 127, 0) - down, 1)
    scale = np.exp2(byte - 127.0)
    codes = (blocks / scale).astype(np.float32).astype(dtype).astype(np.float64)
    return np.moveaxis((codes * scale).reshape(v.shape), -1, axis)


WIDE = False


def mx_kscale(k):
    if not WIDE:
        return np.ones(k)
    levels = np.array([10, -10, 5, -5, 0])
    if k % 512:
        return np.exp2(np.random.permutation(np.resize(levels, k // 32))).repeat(32)
    a = np.empty((k // 512, 16))
    for p in range(k // 512):
        a[p, :8] = np.random.permutation(np.resize(levels, 8))
        for g in range(8):
            far = levels[np.abs(levels - a[p, g]) >= 10]
            a[p, g + 8] = far[np.random.randint(len(far))]
    return np.exp2(a.ravel()).repeat(32)


BF16 = ml_dtypes.bfloat16


def bf(x):
    return np.asarray(x, np.float32).astype(BF16)


def f64(x):
    return np.asarray(x).astype(np.float64)


B, T, D, F = 32, 128, 512, 256
K2, K3, K4 = 2, 3, 4
EPS = 1e-12


def conv_branch(xq, w, b):
    kw = w.shape[1]
    n = xq.shape[1] - kw + 1
    wq = mxq(f64(w), 2, "e4m3")
    out = sum((xq[:, k:k + n, :] @ wq[:, k, :].T) for k in range(kw))
    return np.maximum(out + f64(b), 0.0)


def l2norm(x, axis):
    n = np.sqrt(np.sum(x * x, axis=axis, keepdims=True))
    return x / np.maximum(n, EPS)


def setup_inputs():
    s = mx_kscale(D)
    return {"words_emb": bf(np.random.standard_normal((B, T, D)) * s),
            "W2": bf(np.random.standard_normal((F, K2, D)) / np.sqrt(K2 * D) / s), "b2": bf(np.random.standard_normal(F) * 0.3),
            "W3": bf(np.random.standard_normal((F, K3, D)) / np.sqrt(K3 * D) / s), "b3": bf(np.random.standard_normal(F) * 0.3),
            "W4": bf(np.random.standard_normal((F, K4, D)) / np.sqrt(K4 * D) / s), "b4": bf(np.random.standard_normal(F) * 0.3)}


def reference(words_emb, W2, b2, W3, b3, W4, b4):
    xq = mxq(f64(words_emb), 2, "e4m3")
    a = conv_branch(xq, W2, b2)
    b_ = conv_branch(xq, W3, b3)
    c = conv_branch(xq, W4, b4)
    seq = T - K4 + 1
    main = np.maximum(np.maximum(a[:, :seq], b_[:, :seq]), c[:, :seq])
    pen = np.maximum(a[:, seq], b_[:, seq])[:, None]
    last = a[:, seq + 1][:, None]
    code = np.concatenate([main, pen, last], axis=1)
    code = l2norm(code, 2)
    return code.transpose(0, 2, 1)

@@ -1,0 +1,376 @@
+from contextlib import ExitStack
+
+import concourse.mybir as mybir
+from concourse.masks import make_identity
+
+F32 = mybir.dt.float32
+BF16 = mybir.dt.bfloat16
+U32 = mybir.dt.uint32
+U8 = mybir.dt.uint8
+FP8X4 = mybir.dt.float8_e4m3fn_x4
+ACT = mybir.ActivationFunctionType
+ALU = mybir.AluOpType
+
+P = 128
+B, T, D, F = 32, 128, 512, 256
+WIDTHS = (4, 3, 2)
+NB = 4
+G = B // NB
+L = 8
+PH = T // L
+BLK = NB * PH
+HALO = 4
+NCOL = (L + HALO) * BLK
+GC = NB * T
+UNIT0 = {4: 0, 3: 4, 2: 7}
+BIAS_COL = {4: 0, 3: 2, 2: 4}
+QUANT_RUNS = {4: ((0, 4),), 3: ((0, 2), (2, 1)), 2: ((0, 2),)}
+FLOPS = 2 * B * D * F * (2 * 127 + 3 * 126 + 4 * 125)
+
+
+def tile_textheading_pa_t_kernel(tc, words_emb, W2, b2, W3, b3, W4, b4, out):
+    nc = tc.nc
+    w_dram = {2: W2, 3: W3, 4: W4}
+    b_dram = {2: b2, 3: b3, 4: b4}
+    with ExitStack() as ctx:
+        const = ctx.enter_context(tc.tile_pool(name="const", bufs=1))
+        raw = ctx.enter_context(tc.tile_pool(name="raw", bufs=1))
+        xq = ctx.enter_context(tc.tile_pool(name="xq", bufs=3))
+        xg = ctx.enter_context(tc.tile_pool(name="xg", bufs=2))
+        code_pool = ctx.enter_context(tc.tile_pool(name="code", bufs=4))
+        work = ctx.enter_context(tc.tile_pool(name="work", bufs=2))
+        split = ctx.enter_context(tc.tile_pool(name="split", bufs=3))
+        outp = ctx.enter_context(tc.tile_pool(name="outp", bufs=3))
+        mxp = ctx.enter_context(tc.psum_pool(name="mxp", bufs=2))
+        aux = ctx.enter_context(tc.psum_pool(name="aux", bufs=2))
+        ctx.enter_context(tc.manual_schedule())
+
+        bias_words = const.tile([P, P], F32, name="bias_words")
+        nc.vector.memset(bias_words[:], 0.0)
+        for K in WIDTHS:
+            row = BIAS_COL[K] // 2
+            nc.scalar.dma_start(
+                out=bias_words[row : row + 1, :], in_=b_dram[K].bitcast(F32).rearrange("(o m) -> o m", o=1)
+            )
+        x_raw = {}
+        w_raw = {}
+
+        def load_x(g):
+            t = raw.tile([P, NB, D], BF16, name="x_raw%d" % g)
+            nc.sync.dma_start(out=t[:], in_=words_emb[g * NB : (g + 1) * NB].rearrange("n p d -> p n d"))
+            x_raw[g] = t
+
+        def load_w(h):
+            for K in WIDTHS:
+                t = raw.tile([P, K * D], BF16, name="w_raw%d_%d" % (K, h))
+                nc.sync.dma_start(out=t[:], in_=w_dram[K].rearrange("(m h) k d -> h m (k d)", h=2)[h])
+                w_raw[(K, h)] = t
+
+        load_x(0)
+        load_w(0)
+        load_x(1)
+        load_w(1)
+        for g in range(2, G):
+            load_x(g)
+
+        one_col = const.tile([P, 1], F32, name="one_col")
+        nc.vector.memset(one_col[:], 1.0)
+        dummy = const.tile([P, 1], F32, name="dummy")
+        nc.scalar.activation(out=dummy[:], in_=one_col[:], func=ACT.Abs_reciprocal_sqrt)
+        ident = const.tile([P, P], F32, name="ident")
+        make_identity(nc, ident[:])
+        perm = const.tile([P, P], F32, name="perm")
+        nc.vector.tensor_copy(
+            out=perm[:].rearrange("i (pl ph) -> i pl ph", pl=L), in_=ident[:].rearrange("i (ph pl) -> i pl ph", pl=L)
+        )
+        ones_bf = const.tile([P, P], BF16, name="ones_bf")
+        nc.vector.memset(ones_bf[:], 1.0)
+        ones_f32 = const.tile([P, P], F32, name="ones_f32")
+        nc.vector.memset(ones_f32[:], 1.0)
+        halos = []
+        for i in range(2):
+            halo = const.tile([P, HALO * BLK * 4], BF16, name="halo%d" % i, align_bytes=64)
+            nc.vector.memset(halo[:], 0.0)
+            halos.append(halo)
+
+        w_codes = const.tile([P, 18 * P], U32, name="w_codes", align_bytes=64)
+        w_scales = const.tile([P, 18 * P], U8, name="w_scales", align_bytes=64)
+        bias_sb = const.tile([P, 6], F32, name="bias_sb")
+        bias_pairs = const.tile([P, 3], F32, name="bias_pairs")
+
+        bank_tags = ["c4", "c3", "c2"]
+        bank_no = [0]
+
+        def prep_w(h, widths=WIDTHS):
+            for K in widths:
+                words = w_raw[(K, h)][:].bitcast(F32)
+                grp = raw.tile([P, K * D], BF16, name="w_grp%d_%d" % (K, h), align_bytes=64)
+                grp_w = grp[:].bitcast(F32).rearrange("q (c f u) -> q c f u", c=K, f=P, u=2)
+                for k0 in range(0, K, 2):
+                    cnt = min(2, K - k0)
+                    ps = mxp.tile([P, 4, P], F32, name="ps_w", tag=bank_tags[bank_no[0] % 3])
+                    for i in range(cnt):
+                        for u in range(2):
+                            col = (k0 + i) * 256
+                            nc.tensor.transpose(ps[:, 2 * i + u, :], words[:, col + u : col + 256 : 2], ident[:])
+                    src = ps[:, 0 : 2 * cnt, :].rearrange("q (c u) f -> q c f u", u=2)
+                    if k0 == 0:
+                        nc.scalar.copy(out=grp_w[:, k0 : k0 + cnt], in_=src)
+                    else:
+                        nc.vector.tensor_copy(out=grp_w[:, k0 : k0 + cnt], in_=src)
+                    bank_no[0] += 1
+                unit = h * 9 + UNIT0[K]
+                for k0, cnt in QUANT_RUNS[K]:
+                    cols = slice((unit + k0) * P, (unit + k0 + cnt) * P)
+                    nc.vector.quantize_mx(
+                        out=w_codes[:, cols].bitcast(FP8X4),
+                        scales=w_scales[:, cols],
+                        in_=grp[:, k0 * D : (k0 + cnt) * D],
+                    )
+
+        ps_x = {}
+        x_grp = {}
+        x_codes = {}
+        x_scales = {}
+
+        def transposes_x(g):
+            words = x_raw[g][:].bitcast(F32)
+            banks = []
+            for n0 in range(0, NB, 2):
+                ps = aux.tile([P, 4, P], F32, name="ps_x", tag="aux")
+                for i in range(2):
+                    for u in range(2):
+                        nc.tensor.transpose(ps[:, 2 * i + u, :], words[:, n0 + i, u : 256 : 2], perm[:])
+                banks.append(ps)
+            ps_x[g] = banks
+
+        def evac_x(g, both=False):
+            grp = xg.tile([P, L * BLK * 4], BF16, name="x_grp", align_bytes=64)
+            grp_v = grp[:].bitcast(F32).rearrange("q (pl n ph u) -> q pl n ph u", pl=L, n=NB, ph=PH, u=2)
+            for n in range(NB):
+                i = n % 2
+                dst = grp_v[:, :, n, :, :]
+                src = ps_x[g][n // 2][:, 2 * i : 2 * i + 2, :].rearrange("q u (pl ph) -> q pl ph u", pl=L)
+                if both and n >= 2:
+                    nc.vector.tensor_copy(out=dst, in_=src)
+                else:
+                    nc.scalar.copy(out=dst, in_=src)
+            x_grp[g] = grp
+            x_codes[g] = xq.tile([P, NCOL], U32, name="x_codes", align_bytes=64)
+            x_scales[g] = xq.tile([P, NCOL], U8, name="x_scales", align_bytes=64)
+
+        def quant_x_main(g):
+            nc.vector.quantize_mx(
+                out=x_codes[g][:, 0 : L * BLK].bitcast(FP8X4), scales=x_scales[g][:, 0 : L * BLK], in_=x_grp[g][:]
+            )
+
+        def halo_copy(g):
+            rows = 3 * NB
+            nc.scalar.copy(
+                out=halos[g % 2][:].bitcast(F32).rearrange("q (r w) -> q r w", w=2 * PH)[:, 0:rows, 0 : 2 * PH - 2],
+                in_=x_grp[g][:].bitcast(F32).rearrange("q (r w) -> q r w", w=2 * PH)[:, 0:rows, 2 : 2 * PH],
+            )
+
+        def quant_x_halo(g):
+            nc.vector.quantize_mx(
+                out=x_codes[g][:, L * BLK : NCOL].bitcast(FP8X4),
+                scales=x_scales[g][:, L * BLK : NCOL],
+                in_=halos[g % 2][:],
+            )
+
+        accs = {}
+        codes = {}
+
+        def passes(g, h, K):
+            acc = mxp.tile([P, 512], F32, name="acc", tag="c%d" % K)
+            for k in range(K):
+                unit = h * 9 + UNIT0[K] + k
+                nc.tensor.matmul_mx(
+                    out=acc[:],
+                    lhsT=w_codes[:, unit * P : (unit + 1) * P].bitcast(FP8X4),
+                    lhsT_scale=w_scales[:, unit * P : (unit + 1) * P],
+                    rhs=x_codes[g][:, k * BLK : k * BLK + 512].bitcast(FP8X4),
+                    rhs_scale=x_scales[g][:, k * BLK : k * BLK + 512],
+                    start=(k == 0),
+                    stop=(k == K - 1),
+                )
+            accs[(g, h, K)] = acc
+
+        def relu4(g, h):
+            code = code_pool.tile([P, GC], F32, name="code%d" % h)
+            codes[(g, h)] = code
+            nc.scalar.activation(
+                out=code[:].rearrange("f (m a b) -> f a m b", a=L // 4, b=4),
+                in_=accs[(g, h, 4)][:].rearrange("f (a b m) -> f a m b", a=L // 4, b=4),
+                func=ACT.Relu,
+                bias=bias_sb[:, BIAS_COL[4] + h : BIAS_COL[4] + h + 1],
+            )
+
+        def merge(g, h, K, pieces=1):
+            code = codes[(g, h)]
+            nc.vector.memset(code[:].rearrange("f (n p) -> f n p", p=T)[:, :, T - K : T], 0.0)
+            code_v = code[:].rearrange("f (m pl) -> f m pl", pl=L)
+            acc_v = accs[(g, h, K)][:].rearrange("f (pl m) -> f m pl", pl=L)
+            step = BLK // pieces
+            for c in range(pieces):
+                ms = slice(c * step, (c + 1) * step)
+                for a in range(0, L, 4):
+                    nc.vector.scalar_tensor_tensor(
+                        out=code_v[:, ms, a : a + 4],
+                        in0=acc_v[:, ms, a : a + 4],
+                        scalar=bias_sb[:, BIAS_COL[K] + h : BIAS_COL[K] + h + 1],
+                        in1=code_v[:, ms, a : a + 4],
+                        op0=ALU.add,
+                        op1=ALU.max,
+                    )
+
+        sqs = {}
+        tots = {}
+        his = {}
+        los = {}
+        rinvs = {}
+        sss = {}
+
+        def square(g, h, cs=slice(0, GC)):
+            if (g, h) not in sqs:
+                sqs[(g, h)] = work.tile([P, GC], F32, name="sq%d" % h)
+            nc.scalar.activation(out=sqs[(g, h)][:, cs], in_=codes[(g, h)][:, cs], func=ACT.Square)
+
+        def add_halves(g):
+            tots[g] = work.tile([P, GC], F32, name="tot")
+            nc.gpsimd.tensor_tensor(out=tots[g][:], in0=sqs[(g, 0)][:], in1=sqs[(g, 1)][:], op=ALU.add)
+
+        def high_part(g):
+            his[g] = split.tile([P, GC], BF16, name="hi")
+            nc.gpsimd.tensor_scalar(
+                out=his[g][:], in0=tots[g][:], scalar1=1.0, scalar2=0.0, op0=ALU.mult, op1=ALU.add
+            )
+
+        def low_part(g):
+            los[g] = split.tile([P, GC], BF16, name="lo")
+            nc.gpsimd.tensor_tensor(out=los[g][:], in0=tots[g][:], in1=his[g][:], op=ALU.subtract)
+
+        def sum_filters(g):
+            ss = aux.tile([P, GC], F32, name="ss", tag="aux")
+            nc.tensor.matmul(out=ss[:], lhsT=ones_bf[:], rhs=his[g][:], start=True, stop=False)
+            nc.tensor.matmul(out=ss[:], lhsT=ones_bf[:], rhs=los[g][:], start=False, stop=True)
+            sss[g] = ss
+
+        def rsqrt(g):
+            rinvs[g] = work.tile([P, GC], F32, name="rinv")
+            nc.scalar.activation(out=rinvs[g][:], in_=sss[g][:], func=ACT.Abs_reciprocal_sqrt)
+
+        outs = {}
+
+        def scale_store(g, h):
+            if h == 0:
+                outs[g] = outp.tile([P, NB, 2, T - 1], F32, name="o")
+            o = outs[g]
+            nc.vector.scalar_tensor_tensor(
+                out=o[:, :, h, :],
+                in0=rinvs[g][:].rearrange("f (n p) -> f n p", p=T)[:, :, 0 : T - 1],
+                scalar=1.0e12,
+                in1=codes[(g, h)][:].rearrange("f (n p) -> f n p", p=T)[:, :, 0 : T - 1],
+                op0=ALU.min,
+                op1=ALU.mult,
+            )
+            if h == 1:
+                nc.sync.dma_start(
+                    out=out[g * NB : (g + 1) * NB].rearrange("n (m h) p -> m n (h p)", h=2),
+                    in_=o[:].rearrange("m n h p -> m n (h p)"),
+                )
+
+        transposes_x(0)
+        evac_x(0, both=True)
+        quant_x_main(0)
+        halo_copy(0)
+        prep_w(0, (4,))
+        quant_x_halo(0)
+        prep_w(0, (3, 2))
+        ps_b = aux.tile([P, P], F32, name="ps_b", tag="aux")
+        nc.tensor.transpose(ps_b[:], bias_words[:], ident[:])
+        nc.vector.tensor_copy(out=bias_pairs[:], in_=ps_b[:, 0:3])
+        nc.vector.tensor_copy(out=bias_sb[:], in_=bias_pairs[:].bitcast(BF16))
+
+        for g in range(G):
+            ahead = g >= 1 and g + 1 < G
+            passes(g, 0, 4)
+            if ahead:
+                evac_x(g + 1)
+            passes(g, 0, 3)
+            passes(g, 0, 2)
+            relu4(g, 0)
+            if ahead:
+                quant_x_main(g + 1)
+                halo_copy(g + 1)
+            if g >= 1:
+                square(g - 1, 1)
+                add_halves(g - 1)
+                high_part(g - 1)
+                low_part(g - 1)
+            merge(g, 0, 3)
+            if ahead:
+                quant_x_halo(g + 1)
+            merge(g, 0, 2)
+            if g == 0:
+                transposes_x(1)
+                evac_x(1)
+                prep_w(1)
+                quant_x_main(1)
+                halo_copy(1)
+            if g >= 2:
+                sum_filters(g - 2)
+                rsqrt(g - 2)
+            passes(g, 1, 4)
+            passes(g, 1, 3)
+            passes(g, 1, 2)
+            if g >= 2:
+                scale_store(g - 2, 0)
+                scale_store(g - 2, 1)
+            relu4(g, 1)
+            square(g, 0)
+            merge(g, 1, 3)
+            if g == 0:
+                quant_x_halo(1)
+            merge(g, 1, 2, pieces=(2 if g == G - 1 else 1))
+            if g + 2 < G:
+                transposes_x(g + 2)
+
+        sum_filters(G - 2)
+        rsqrt(G - 2)
+        g = G - 1
+        half = GC // 2
+        last_ss = []
+        for c in range(2):
+            ss = aux.tile([P, half], F32, name="ss_last", tag="aux")
+            nc.tensor.matmul(
+                out=ss[:], lhsT=ones_f32[:], rhs=sqs[(g, 0)][:, c * half : (c + 1) * half], start=True, stop=False
+            )
+            last_ss.append(ss)
+        for c in range(2):
+            square(g, 1, slice(c * half, (c + 1) * half))
+        scale_store(G - 2, 0)
+        scale_store(G - 2, 1)
+        rinv = work.tile([P, GC], F32, name="rinv")
+        for c in range(2):
+            cs = slice(c * half, (c + 1) * half)
+            nc.tensor.matmul(out=last_ss[c][:], lhsT=ones_f32[:], rhs=sqs[(g, 1)][:, cs], start=False, stop=True)
+            nc.scalar.activation(out=rinv[:, cs], in_=last_ss[c][:], func=ACT.Abs_reciprocal_sqrt)
+        for c in range(2):
+            cs = slice(c * half, (c + 1) * half)
+            o = outp.tile([P, NB // 2, 2, T - 1], F32, name="o_last")
+            for h in range(2):
+                nc.vector.scalar_tensor_tensor(
+                    out=o[:, :, h, :],
+                    in0=rinv[:, cs].rearrange("f (n p) -> f n p", p=T)[:, :, 0 : T - 1],
+                    scalar=1.0e12,
+                    in1=codes[(g, h)][:, cs].rearrange("f (n p) -> f n p", p=T)[:, :, 0 : T - 1],
+                    op0=ALU.min,
+                    op1=ALU.mult,
+                )
+            n0 = g * NB + c * (NB // 2)
+            queue = nc.sync if c == 0 else nc.scalar
+            queue.dma_start(
+                out=out[n0 : n0 + NB // 2].rearrange("n (m h) p -> m n (h p)", h=2),
+                in_=o[:].rearrange("m n h p -> m n (h p)"),
+            )

@@ -6,6 +6,7 @@ from concourse.masks import make_identity
 F32 = mybir.dt.float32
 BF16 = mybir.dt.bfloat16
 U32 = mybir.dt.uint32
+I32 = mybir.dt.int32
 U8 = mybir.dt.uint8
 FP8X4 = mybir.dt.float8_e4m3fn_x4
 ACT = mybir.ActivationFunctionType
@@ -16,16 +17,14 @@ B, T, D, F = 32, 128, 512, 256
 WIDTHS = (4, 3, 2)
 NB = 4
 G = B // NB
-L = 8
+LAST = G - 1
+L = 4
 PH = T // L
-BLK = NB * PH
-HALO = 4
-NCOL = (L + HALO) * BLK
-GC = NB * T
 UNIT0 = {4: 0, 3: 4, 2: 7}
 BIAS_COL = {4: 0, 3: 2, 2: 4}
-QUANT_RUNS = {4: ((0, 4),), 3: ((0, 2), (2, 1)), 2: ((0, 2),)}
+NCOL = 1024
 FLOPS = 2 * B * D * F * (2 * 127 + 3 * 126 + 4 * 125)
+WARM = 4
 
 
 def tile_textheading_pa_t_kernel(tc, words_emb, W2, b2, W3, b3, W4, b4, out):
@@ -35,14 +34,13 @@ def tile_textheading_pa_t_kernel(tc, words_emb, W2, b2, W3, b3, W4, b4, out):
     with ExitStack() as ctx:
         const = ctx.enter_context(tc.tile_pool(name="const", bufs=1))
         raw = ctx.enter_context(tc.tile_pool(name="raw", bufs=1))
-        xq = ctx.enter_context(tc.tile_pool(name="xq", bufs=3))
-        xg = ctx.enter_context(tc.tile_pool(name="xg", bufs=2))
-        code_pool = ctx.enter_context(tc.tile_pool(name="code", bufs=4))
-        work = ctx.enter_context(tc.tile_pool(name="work", bufs=2))
+        xg = ctx.enter_context(tc.tile_pool(name="xg", bufs=3))
+        code_pool = ctx.enter_context(tc.tile_pool(name="code", bufs=5))
+        work = ctx.enter_context(tc.tile_pool(name="work", bufs=3))
         split = ctx.enter_context(tc.tile_pool(name="split", bufs=3))
         outp = ctx.enter_context(tc.tile_pool(name="outp", bufs=3))
-        mxp = ctx.enter_context(tc.psum_pool(name="mxp", bufs=2))
-        aux = ctx.enter_context(tc.psum_pool(name="aux", bufs=2))
+        mxp = ctx.enter_context(tc.psum_pool(name="mxp", bufs=5))
+        aux = ctx.enter_context(tc.psum_pool(name="aux", bufs=3))
         ctx.enter_context(tc.manual_schedule())
 
         bias_words = const.tile([P, P], F32, name="bias_words")
@@ -54,175 +52,240 @@ def tile_textheading_pa_t_kernel(tc, words_emb, W2, b2, W3, b3, W4, b4, out):
             )
         x_raw = {}
         w_raw = {}
+        w_tile = {}
 
-        def load_x(g):
-            t = raw.tile([P, NB, D], BF16, name="x_raw%d" % g)
-            nc.sync.dma_start(out=t[:], in_=words_emb[g * NB : (g + 1) * NB].rearrange("n p d -> p n d"))
+        def load_x(g, pieces=1):
+            t = raw.tile([P, L, D], BF16, name="x_raw%d" % g)
+            src = words_emb[g * NB : (g + 1) * NB].rearrange("n (ph l) d -> (n ph) l d", l=L)
+            step = L // pieces
+            for l in range(0, L, step):
+                nc.sync.dma_start(out=t[:, l : l + step, :], in_=src[:, l : l + step, :])
             x_raw[g] = t
 
-        def load_w(h):
-            for K in WIDTHS:
-                t = raw.tile([P, K * D], BF16, name="w_raw%d_%d" % (K, h))
-                nc.sync.dma_start(out=t[:], in_=w_dram[K].rearrange("(m h) k d -> h m (k d)", h=2)[h])
-                w_raw[(K, h)] = t
+        def load_w(K, h, k0, cnt):
+            t = raw.tile([P, cnt * D], BF16, name="w_raw%d_%d_%d" % (K, h, k0))
+            src = w_dram[K].rearrange("(m h) k d -> h m k d", h=2)[h]
+            nc.sync.dma_start(
+                out=t[:].rearrange("m (k d) -> m k d", k=cnt), in_=src[:, k0 : k0 + cnt, :]
+            )
+            for k in range(cnt):
+                w_raw[(K, h, k0 + k)] = t[:, k * D : (k + 1) * D]
+                w_tile[(K, h, k0 + k)] = t[:, k * D : cnt * D]
 
-        load_x(0)
-        load_w(0)
+        load_x(0, pieces=2)
+        load_w(4, 0, 0, 2)
+        load_w(4, 0, 2, 2)
+        load_w(3, 0, 0, 3)
+        load_w(2, 0, 0, 2)
         load_x(1)
-        load_w(1)
+        load_w(4, 1, 0, 4)
+        load_w(3, 1, 0, 3)
+        load_w(2, 1, 0, 2)
         for g in range(2, G):
             load_x(g)
 
+        warm = const.tile([P, 512], BF16, name="warm")
+        nc.vector.memset(warm[:], 0.0)
         one_col = const.tile([P, 1], F32, name="one_col")
         nc.vector.memset(one_col[:], 1.0)
         dummy = const.tile([P, 1], F32, name="dummy")
         nc.scalar.activation(out=dummy[:], in_=one_col[:], func=ACT.Abs_reciprocal_sqrt)
         ident = const.tile([P, P], F32, name="ident")
         make_identity(nc, ident[:])
-        perm = const.tile([P, P], F32, name="perm")
-        nc.vector.tensor_copy(
-            out=perm[:].rearrange("i (pl ph) -> i pl ph", pl=L), in_=ident[:].rearrange("i (ph pl) -> i pl ph", pl=L)
-        )
+        zeros = const.tile([P, NB * 3], F32, name="zeros")
+        nc.vector.memset(zeros[:], 0.0)
         ones_bf = const.tile([P, P], BF16, name="ones_bf")
         nc.vector.memset(ones_bf[:], 1.0)
         ones_f32 = const.tile([P, P], F32, name="ones_f32")
         nc.vector.memset(ones_f32[:], 1.0)
-        halos = []
-        for i in range(2):
-            halo = const.tile([P, HALO * BLK * 4], BF16, name="halo%d" % i, align_bytes=64)
-            nc.vector.memset(halo[:], 0.0)
-            halos.append(halo)
+        planes = []
+        for i in range(3):
+            c = const.tile([P, NCOL], U32, name="x_codes%d" % i, align_bytes=64)
+            s = const.tile([P, NCOL], U8, name="x_scales%d" % i, align_bytes=64)
+            nc.gpsimd.memset(s[:].bitcast(U32), 0)
+            planes.append((c, s))
 
         w_codes = const.tile([P, 18 * P], U32, name="w_codes", align_bytes=64)
         w_scales = const.tile([P, 18 * P], U8, name="w_scales", align_bytes=64)
         bias_sb = const.tile([P, 6], F32, name="bias_sb")
         bias_pairs = const.tile([P, 3], F32, name="bias_pairs")
 
-        bank_tags = ["c4", "c3", "c2"]
-        bank_no = [0]
+        ps_warm = aux.tile([P, 512], F32, name="ps_warm", tag="aux")
 
-        def prep_w(h, widths=WIDTHS):
-            for K in widths:
-                words = w_raw[(K, h)][:].bitcast(F32)
-                grp = raw.tile([P, K * D], BF16, name="w_grp%d_%d" % (K, h), align_bytes=64)
-                grp_w = grp[:].bitcast(F32).rearrange("q (c f u) -> q c f u", c=K, f=P, u=2)
-                for k0 in range(0, K, 2):
-                    cnt = min(2, K - k0)
-                    ps = mxp.tile([P, 4, P], F32, name="ps_w", tag=bank_tags[bank_no[0] % 3])
-                    for i in range(cnt):
-                        for u in range(2):
-                            col = (k0 + i) * 256
-                            nc.tensor.transpose(ps[:, 2 * i + u, :], words[:, col + u : col + 256 : 2], ident[:])
-                    src = ps[:, 0 : 2 * cnt, :].rearrange("q (c u) f -> q c f u", u=2)
-                    if k0 == 0:
-                        nc.scalar.copy(out=grp_w[:, k0 : k0 + cnt], in_=src)
+        def warm_up(count):
+            for i in range(count):
+                nc.tensor.matmul(out=ps_warm[:], lhsT=warm[:, 0:P], rhs=warm[:], start=True, stop=True)
+
+        w_grp = {}
+        w_ord = {}
+
+        def order_w(K, h, k0, cnt, eng="s"):
+            t = raw.tile([P, cnt, 2, P], F32, name="w_ord%d_%d_%d" % (K, h, k0))
+            for k in range(cnt):
+                w_ord[(K, h, k0 + k)] = t[:, k]
+            src = w_tile[(K, h, k0)][:, 0 : cnt * D].bitcast(F32).rearrange("m (k q u) -> m k u q", k=cnt, u=2)
+            if eng == "s":
+                nc.scalar.copy(out=t[:], in_=src)
+            else:
+                nc.vector.tensor_copy(out=t[:], in_=src)
+
+        def trans_w(K, h, k0, cnt, eng):
+            if (K, h) not in w_grp:
+                w_grp[(K, h)] = raw.tile([P, K * D], BF16, name="w_grp%d_%d" % (K, h), align_bytes=64)
+            grp_w = w_grp[(K, h)][:].bitcast(F32).rearrange("q (c f u) -> q c f u", c=K, f=P, u=2)
+            ps = mxp.tile([P, 4, P], F32, name="ps_w", tag="acc")
+            for i in range(cnt):
+                words = w_raw[(K, h, k0 + i)].bitcast(F32)
+                for u in range(2):
+                    if (K, h, k0 + i) in w_ord:
+                        src = w_ord[(K, h, k0 + i)][:, u, :]
                     else:
-                        nc.vector.tensor_copy(out=grp_w[:, k0 : k0 + cnt], in_=src)
-                    bank_no[0] += 1
-                unit = h * 9 + UNIT0[K]
-                for k0, cnt in QUANT_RUNS[K]:
-                    cols = slice((unit + k0) * P, (unit + k0 + cnt) * P)
-                    nc.vector.quantize_mx(
-                        out=w_codes[:, cols].bitcast(FP8X4),
-                        scales=w_scales[:, cols],
-                        in_=grp[:, k0 * D : (k0 + cnt) * D],
-                    )
+                        src = words[:, u : 256 : 2]
+                    nc.tensor.transpose(ps[:, 2 * i + u, :], src, ident[:])
+            src = ps[:, 0 : 2 * cnt, :].rearrange("q (c u) f -> q c f u", u=2)
+            if eng == "s":
+                nc.scalar.copy(out=grp_w[:, k0 : k0 + cnt], in_=src)
+            else:
+                nc.vector.tensor_copy(out=grp_w[:, k0 : k0 + cnt], in_=src)
+
+        def quant_w(K, h, k0, cnt):
+            unit = h * 9 + UNIT0[K]
+            cols = slice((unit + k0) * P, (unit + k0 + cnt) * P)
+            nc.vector.quantize_mx(
+                out=w_codes[:, cols].bitcast(FP8X4),
+                scales=w_scales[:, cols],
+                in_=w_grp[(K, h)][:, k0 * D : (k0 + cnt) * D],
+            )
 
         ps_x = {}
         x_grp = {}
-        x_codes = {}
-        x_scales = {}
+        x_ord = {}
 
-        def transposes_x(g):
-            words = x_raw[g][:].bitcast(F32)
-            banks = []
-            for n0 in range(0, NB, 2):
+        def order_x(g, half):
+            if half == 0:
+                x_ord[g] = xg.tile([P, L, 2, P], F32, name="x_ord")
+            ls = slice(2 * half, 2 * half + 2)
+            words = x_raw[g][:].rearrange("m l d -> m (l d)").bitcast(F32).rearrange("m (l q u) -> m l u q", l=L, u=2)
+            nc.scalar.copy(out=x_ord[g][:, ls], in_=words[:, ls])
+
+        def transposes_x(g, parts=(0, 1)):
+            banks = ps_x.setdefault(g, [])
+            for i in parts:
                 ps = aux.tile([P, 4, P], F32, name="ps_x", tag="aux")
-                for i in range(2):
+                for c in range(2):
+                    words = x_raw[g][:, 2 * i + c, :].bitcast(F32)
                     for u in range(2):
-                        nc.tensor.transpose(ps[:, 2 * i + u, :], words[:, n0 + i, u : 256 : 2], perm[:])
+                        src = x_ord[g][:, 2 * i + c, u, :] if g in x_ord else words[:, u : 256 : 2]
+                        nc.tensor.transpose(ps[:, 2 * c + u, :], src, ident[:])
                 banks.append(ps)
-            ps_x[g] = banks
 
-        def evac_x(g, both=False):
-            grp = xg.tile([P, L * BLK * 4], BF16, name="x_grp", align_bytes=64)
-            grp_v = grp[:].bitcast(F32).rearrange("q (pl n ph u) -> q pl n ph u", pl=L, n=NB, ph=PH, u=2)
-            for n in range(NB):
-                i = n % 2
-                dst = grp_v[:, :, n, :, :]
-                src = ps_x[g][n // 2][:, 2 * i : 2 * i + 2, :].rearrange("q u (pl ph) -> q pl ph u", pl=L)
-                if both and n >= 2:
-                    nc.vector.tensor_copy(out=dst, in_=src)
-                else:
-                    nc.scalar.copy(out=dst, in_=src)
-            x_grp[g] = grp
-            x_codes[g] = xq.tile([P, NCOL], U32, name="x_codes", align_bytes=64)
-            x_scales[g] = xq.tile([P, NCOL], U8, name="x_scales", align_bytes=64)
+        def subs(g):
+            if g < LAST:
+                return ((g * NB, NB, 0, P),)
+            return ((g * NB, NB // 2, 0, P // 2), (g * NB + NB // 2, NB // 2, 512, P // 2))
 
-        def quant_x_main(g):
+        def evac_x(g, engines="ss", parts=(0, 1)):
+            if g not in x_grp:
+                x_grp[g] = xg.tile([P, 512 * 4], BF16, name="x_grp", align_bytes=64)
+            grp = x_grp[g]
+            ns = len(subs(g))
+            dst = grp[:].bitcast(F32).rearrange("q (s l m u) -> q s l m u", s=ns, l=L, u=2)
+            for i in parts:
+                src = ps_x[g][i][:].rearrange("q (c u) (s m) -> q s c m u", u=2, s=ns)
+                for s in range(ns):
+                    if engines[i] == "v":
+                        nc.vector.tensor_copy(out=dst[:, s, 2 * i : 2 * i + 2], in_=src[:, s])
+                    else:
+                        nc.scalar.copy(out=dst[:, s, 2 * i : 2 * i + 2], in_=src[:, s])
+
+        def quant_half(g, i):
+            codes, scales = planes[g % 3]
+            cols = slice(i * 256, (i + 1) * 256)
             nc.vector.quantize_mx(
-                out=x_codes[g][:, 0 : L * BLK].bitcast(FP8X4), scales=x_scales[g][:, 0 : L * BLK], in_=x_grp[g][:]
+                out=codes[:, cols].bitcast(FP8X4), scales=scales[:, cols], in_=x_grp[g][:, i * 1024 : (i + 1) * 1024]
             )
 
-        def halo_copy(g):
-            rows = 3 * NB
-            nc.scalar.copy(
-                out=halos[g % 2][:].bitcast(F32).rearrange("q (r w) -> q r w", w=2 * PH)[:, 0:rows, 0 : 2 * PH - 2],
-                in_=x_grp[g][:].bitcast(F32).rearrange("q (r w) -> q r w", w=2 * PH)[:, 0:rows, 2 : 2 * PH],
-            )
+        def quant_x(g):
+            codes, scales = planes[g % 3]
+            for s, (n0, nb, c0, blk) in enumerate(subs(g)):
+                w = L * blk
+                nc.vector.quantize_mx(
+                    out=codes[:, c0 : c0 + w].bitcast(FP8X4),
+                    scales=scales[:, c0 : c0 + w],
+                    in_=x_grp[g][:, s * w * 4 : (s + 1) * w * 4],
+                )
 
-        def quant_x_halo(g):
-            nc.vector.quantize_mx(
-                out=x_codes[g][:, L * BLK : NCOL].bitcast(FP8X4),
-                scales=x_scales[g][:, L * BLK : NCOL],
-                in_=halos[g % 2][:],
-            )
+        def halo_codes(g):
+            codes = planes[g % 3][0]
+            for n0, nb, c0, blk in subs(g):
+                w = L * blk
+                r = 3 * blk
+                nc.vector.tensor_copy(
+                    out=codes[:, c0 + w : c0 + w + r].bitcast(I32), in_=codes[:, c0 + 1 : c0 + 1 + r].bitcast(I32)
+                )
+
+        def halo_scales(g):
+            scales = planes[g % 3][1]
+            for n0, nb, c0, blk in subs(g):
+                w = L * blk
+                r = 3 * blk
+                nc.vector.tensor_copy(out=scales[:, c0 + w : c0 + w + r], in_=scales[:, c0 + 1 : c0 + 1 + r])
+
+        def halo(g):
+            halo_codes(g)
+            halo_scales(g)
 
         accs = {}
-        codes = {}
+        code_of = {}
 
-        def passes(g, h, K):
-            acc = mxp.tile([P, 512], F32, name="acc", tag="c%d" % K)
+        def passes(g, h, K, s=0):
+            n0, nb, c0, blk = subs(g)[s]
+            codes, scales = planes[g % 3]
+            acc = mxp.tile([P, L * blk], F32, name="acc", tag="acc")
             for k in range(K):
                 unit = h * 9 + UNIT0[K] + k
+                cols = slice(c0 + k * blk, c0 + (k + L) * blk)
                 nc.tensor.matmul_mx(
                     out=acc[:],
                     lhsT=w_codes[:, unit * P : (unit + 1) * P].bitcast(FP8X4),
                     lhsT_scale=w_scales[:, unit * P : (unit + 1) * P],
-                    rhs=x_codes[g][:, k * BLK : k * BLK + 512].bitcast(FP8X4),
-                    rhs_scale=x_scales[g][:, k * BLK : k * BLK + 512],
+                    rhs=codes[:, cols].bitcast(FP8X4),
+                    rhs_scale=scales[:, cols],
                     start=(k == 0),
                     stop=(k == K - 1),
                 )
-            accs[(g, h, K)] = acc
+            accs[(g, h, K, s)] = acc
 
-        def relu4(g, h):
-            code = code_pool.tile([P, GC], F32, name="code%d" % h)
-            codes[(g, h)] = code
+        def relu4(g, h, s=0):
+            n0, nb, c0, blk = subs(g)[s]
+            code = code_pool.tile([P, nb * T], F32, name="code%d" % h)
+            code_of[(g, h, s)] = code
             nc.scalar.activation(
-                out=code[:].rearrange("f (m a b) -> f a m b", a=L // 4, b=4),
-                in_=accs[(g, h, 4)][:].rearrange("f (a b m) -> f a m b", a=L // 4, b=4),
+                out=code[:].rearrange("f (m l) -> f m l", l=L),
+                in_=accs[(g, h, 4, s)][:].rearrange("f (l m) -> f m l", l=L),
                 func=ACT.Relu,
                 bias=bias_sb[:, BIAS_COL[4] + h : BIAS_COL[4] + h + 1],
             )
+            clear(g, h, 4, s)
 
-        def merge(g, h, K, pieces=1):
-            code = codes[(g, h)]
-            nc.vector.memset(code[:].rearrange("f (n p) -> f n p", p=T)[:, :, T - K : T], 0.0)
-            code_v = code[:].rearrange("f (m pl) -> f m pl", pl=L)
-            acc_v = accs[(g, h, K)][:].rearrange("f (pl m) -> f m pl", pl=L)
-            step = BLK // pieces
-            for c in range(pieces):
-                ms = slice(c * step, (c + 1) * step)
-                for a in range(0, L, 4):
-                    nc.vector.scalar_tensor_tensor(
-                        out=code_v[:, ms, a : a + 4],
-                        in0=acc_v[:, ms, a : a + 4],
-                        scalar=bias_sb[:, BIAS_COL[K] + h : BIAS_COL[K] + h + 1],
-                        in1=code_v[:, ms, a : a + 4],
-                        op0=ALU.add,
-                        op1=ALU.max,
-                    )
+        def clear(g, h, K, s=0):
+            nb = subs(g)[s][1]
+            last = code_of[(g, h, s)][:].rearrange("f (n p) -> f n p", p=T)[:, :, T - K + 1 : T]
+            if K == 4:
+                nc.scalar.copy(out=last, in_=zeros[:, 0 : nb * (K - 1)].rearrange("f (n p) -> f n p", p=K - 1))
+            else:
+                nc.vector.memset(last, 0.0)
+
+        def merge(g, h, K, s=0):
+            code_v = code_of[(g, h, s)][:].rearrange("f (m l) -> f m l", l=L)
+            nc.vector.scalar_tensor_tensor(
+                out=code_v,
+                in0=accs[(g, h, K, s)][:].rearrange("f (l m) -> f m l", l=L),
+                scalar=bias_sb[:, BIAS_COL[K] + h : BIAS_COL[K] + h + 1],
+                in1=code_v,
+                op0=ALU.add,
+                op1=ALU.max,
+            )
 
         sqs = {}
         tots = {}
@@ -230,147 +293,236 @@ def tile_textheading_pa_t_kernel(tc, words_emb, W2, b2, W3, b3, W4, b4, out):
         los = {}
         rinvs = {}
         sss = {}
-
-        def square(g, h, cs=slice(0, GC)):
-            if (g, h) not in sqs:
-                sqs[(g, h)] = work.tile([P, GC], F32, name="sq%d" % h)
-            nc.scalar.activation(out=sqs[(g, h)][:, cs], in_=codes[(g, h)][:, cs], func=ACT.Square)
-
-        def add_halves(g):
-            tots[g] = work.tile([P, GC], F32, name="tot")
-            nc.gpsimd.tensor_tensor(out=tots[g][:], in0=sqs[(g, 0)][:], in1=sqs[(g, 1)][:], op=ALU.add)
-
-        def high_part(g):
-            his[g] = split.tile([P, GC], BF16, name="hi")
-            nc.gpsimd.tensor_scalar(
-                out=his[g][:], in0=tots[g][:], scalar1=1.0, scalar2=0.0, op0=ALU.mult, op1=ALU.add
-            )
-
-        def low_part(g):
-            los[g] = split.tile([P, GC], BF16, name="lo")
-            nc.gpsimd.tensor_tensor(out=los[g][:], in0=tots[g][:], in1=his[g][:], op=ALU.subtract)
-
-        def sum_filters(g):
-            ss = aux.tile([P, GC], F32, name="ss", tag="aux")
-            nc.tensor.matmul(out=ss[:], lhsT=ones_bf[:], rhs=his[g][:], start=True, stop=False)
-            nc.tensor.matmul(out=ss[:], lhsT=ones_bf[:], rhs=los[g][:], start=False, stop=True)
-            sss[g] = ss
-
-        def rsqrt(g):
-            rinvs[g] = work.tile([P, GC], F32, name="rinv")
-            nc.scalar.activation(out=rinvs[g][:], in_=sss[g][:], func=ACT.Abs_reciprocal_sqrt)
-
         outs = {}
 
-        def scale_store(g, h):
+        def cols_of(g, s):
+            return subs(g)[s][1] * T
+
+        def square(g, h, s=0):
+            sqs[(g, h, s)] = work.tile([P, cols_of(g, s)], F32, name="sq%d" % h)
+            nc.scalar.activation(out=sqs[(g, h, s)][:], in_=code_of[(g, h, s)][:], func=ACT.Square)
+
+        def split_sum(g, s=0):
+            tot = work.tile([P, cols_of(g, s)], F32, name="tot")
+            nc.gpsimd.tensor_tensor(out=tot[:], in0=sqs[(g, 0, s)][:], in1=sqs[(g, 1, s)][:], op=ALU.add)
+            hi = split.tile([P, cols_of(g, s)], BF16, name="hi")
+            nc.gpsimd.tensor_scalar(out=hi[:], in0=tot[:], scalar1=1.0, scalar2=0.0, op0=ALU.mult, op1=ALU.add)
+            lo = split.tile([P, cols_of(g, s)], BF16, name="lo")
+            nc.gpsimd.tensor_tensor(out=lo[:], in0=tot[:], in1=hi[:], op=ALU.subtract)
+            his[(g, s)] = hi
+            los[(g, s)] = lo
+
+        def sum_filters(g, s=0):
+            ss = aux.tile([P, cols_of(g, s)], F32, name="ss", tag="aux")
+            nc.tensor.matmul(out=ss[:], lhsT=ones_bf[:], rhs=his[(g, s)][:], start=True, stop=False)
+            nc.tensor.matmul(out=ss[:], lhsT=ones_bf[:], rhs=los[(g, s)][:], start=False, stop=True)
+            sss[(g, s)] = ss
+
+        def sum_f32(g, h, s):
             if h == 0:
-                outs[g] = outp.tile([P, NB, 2, T - 1], F32, name="o")
-            o = outs[g]
+                sss[(g, s)] = aux.tile([P, cols_of(g, s)], F32, name="ss", tag="aux")
+            nc.tensor.matmul(
+                out=sss[(g, s)][:], lhsT=ones_f32[:], rhs=sqs[(g, h, s)][:], start=(h == 0), stop=(h == 1)
+            )
+
+        def rsqrt(g, s=0):
+            rinvs[(g, s)] = work.tile([P, cols_of(g, s)], F32, name="rinv")
+            nc.scalar.activation(out=rinvs[(g, s)][:], in_=sss[(g, s)][:], func=ACT.Abs_reciprocal_sqrt)
+
+        def scale(g, h, s=0):
+            n0, nb, c0, blk = subs(g)[s]
+            if h == 0:
+                outs[(g, s)] = outp.tile([P, nb, 2, T - 1], F32, name="o")
             nc.vector.scalar_tensor_tensor(
-                out=o[:, :, h, :],
-                in0=rinvs[g][:].rearrange("f (n p) -> f n p", p=T)[:, :, 0 : T - 1],
+                out=outs[(g, s)][:, :, h, :],
+                in0=rinvs[(g, s)][:].rearrange("f (n p) -> f n p", p=T)[:, :, 0 : T - 1],
                 scalar=1.0e12,
-                in1=codes[(g, h)][:].rearrange("f (n p) -> f n p", p=T)[:, :, 0 : T - 1],
+                in1=code_of[(g, h, s)][:].rearrange("f (n p) -> f n p", p=T)[:, :, 0 : T - 1],
                 op0=ALU.min,
                 op1=ALU.mult,
             )
             if h == 1:
                 nc.sync.dma_start(
-                    out=out[g * NB : (g + 1) * NB].rearrange("n (m h) p -> m n (h p)", h=2),
-                    in_=o[:].rearrange("m n h p -> m n (h p)"),
+                    out=out[n0 : n0 + nb].rearrange("n (m h) p -> m n (h p)", h=2),
+                    in_=outs[(g, s)][:].rearrange("m n h p -> m n (h p)"),
                 )
 
-        transposes_x(0)
-        evac_x(0, both=True)
-        quant_x_main(0)
-        halo_copy(0)
-        prep_w(0, (4,))
-        quant_x_halo(0)
-        prep_w(0, (3, 2))
+        warm_up(WARM)
+        transposes_x(0, (0,))
+        evac_x(0, "ss", (0,))
+        transposes_x(0, (1,))
+        evac_x(0, "vv", (1,))
+        quant_half(0, 0)
+        trans_w(4, 0, 0, 2, "s")
+        quant_half(0, 1)
+        trans_w(4, 0, 2, 2, "s")
+        quant_w(4, 0, 0, 2)
+        halo(0)
+        quant_w(4, 0, 2, 2)
+        trans_w(3, 0, 0, 2, "s")
+        trans_w(3, 0, 2, 1, "v")
+        quant_w(3, 0, 0, 2)
+        trans_w(2, 0, 0, 2, "s")
         ps_b = aux.tile([P, P], F32, name="ps_b", tag="aux")
         nc.tensor.transpose(ps_b[:], bias_words[:], ident[:])
+        quant_w(3, 0, 2, 1)
         nc.vector.tensor_copy(out=bias_pairs[:], in_=ps_b[:, 0:3])
+        quant_w(2, 0, 0, 2)
         nc.vector.tensor_copy(out=bias_sb[:], in_=bias_pairs[:].bitcast(BF16))
+        order_x(1, 0)
+        passes(0, 0, 4)
+        order_x(1, 1)
+        order_w(4, 1, 0, 2, "v")
+        order_w(4, 1, 2, 2, "v")
+        order_w(3, 1, 2, 1, "v")
+        order_w(3, 1, 0, 2)
+        relu4(0, 0)
+        transposes_x(1)
+        evac_x(1, "sv")
+        passes(0, 0, 3)
+        quant_x(1)
+        passes(0, 0, 2)
+        order_w(2, 1, 0, 2)
+        merge(0, 0, 3)
+        halo(1)
+        trans_w(4, 1, 0, 2, "s")
+        trans_w(4, 1, 2, 2, "s")
+        clear(0, 0, 3)
+        merge(0, 0, 2)
+        quant_w(4, 1, 0, 4)
+        passes(1, 0, 4)
+        relu4(1, 0)
+        trans_w(3, 1, 0, 2, "s")
+        trans_w(3, 1, 2, 1, "v")
+        quant_w(3, 1, 2, 1)
+        quant_w(3, 1, 0, 2)
+        passes(1, 0, 3)
+        order_x(2, 0)
+        merge(1, 0, 3)
+        trans_w(2, 1, 0, 2, "s")
+        square(0, 0)
+        passes(1, 0, 2)
+        quant_w(2, 1, 0, 2)
+        clear(1, 0, 3)
+        merge(1, 0, 2)
+        passes(0, 1, 4)
+        order_x(2, 1)
+        relu4(0, 1)
+        order_x(3, 0)
+        passes(0, 1, 3)
+        merge(0, 1, 3)
+        passes(0, 1, 2)
+        transposes_x(2)
+        clear(0, 1, 3)
+        merge(0, 1, 2)
+        order_x(3, 1)
+        evac_x(2, "sv")
+        passes(1, 1, 4)
+        quant_x(2)
+        relu4(1, 1)
+        square(0, 1)
+        split_sum(0)
+        passes(1, 1, 3)
+        merge(1, 1, 3)
+        halo(2)
+        square(1, 0)
+        passes(1, 1, 2)
+        clear(1, 1, 3)
+        merge(1, 1, 2)
+        order_x(4, 0)
+        order_x(4, 1)
+        transposes_x(3)
 
-        for g in range(G):
-            ahead = g >= 1 and g + 1 < G
+        for g in range(2, LAST):
             passes(g, 0, 4)
-            if ahead:
-                evac_x(g + 1)
-            passes(g, 0, 3)
-            passes(g, 0, 2)
-            relu4(g, 0)
-            if ahead:
-                quant_x_main(g + 1)
-                halo_copy(g + 1)
-            if g >= 1:
-                square(g - 1, 1)
-                add_halves(g - 1)
-                high_part(g - 1)
-                low_part(g - 1)
-            merge(g, 0, 3)
-            if ahead:
-                quant_x_halo(g + 1)
-            merge(g, 0, 2)
-            if g == 0:
-                transposes_x(1)
-                evac_x(1)
-                prep_w(1)
-                quant_x_main(1)
-                halo_copy(1)
-            if g >= 2:
-                sum_filters(g - 2)
+            evac_x(g + 1, "ss", (0,))
+            evac_x(g + 1, "vv", (1,))
+            if g > 2:
                 rsqrt(g - 2)
+            quant_x(g + 1)
+            if g > 2:
+                scale(g - 2, 0)
+                scale(g - 2, 1)
+            relu4(g, 0)
+            square(g - 1, 1)
+            split_sum(g - 1)
+            passes(g, 0, 3)
+            merge(g, 0, 3)
+            halo_scales(g + 1)
+            passes(g, 0, 2)
+            clear(g, 0, 3)
+            merge(g, 0, 2)
+            if g == 2:
+                sum_filters(0)
+                rsqrt(0)
+                scale(0, 0)
+                scale(0, 1)
+            if g + 3 < G:
+                order_x(g + 3, 0)
             passes(g, 1, 4)
-            passes(g, 1, 3)
-            passes(g, 1, 2)
-            if g >= 2:
-                scale_store(g - 2, 0)
-                scale_store(g - 2, 1)
             relu4(g, 1)
             square(g, 0)
+            passes(g, 1, 3)
             merge(g, 1, 3)
-            if g == 0:
-                quant_x_halo(1)
-            merge(g, 1, 2, pieces=(2 if g == G - 1 else 1))
+            halo_codes(g + 1)
+            if g + 3 < G:
+                order_x(g + 3, 1)
+            passes(g, 1, 2)
+            clear(g, 1, 3)
+            merge(g, 1, 2)
             if g + 2 < G:
                 transposes_x(g + 2)
+            sum_filters(g - 1)
 
-        sum_filters(G - 2)
-        rsqrt(G - 2)
-        g = G - 1
-        half = GC // 2
-        last_ss = []
-        for c in range(2):
-            ss = aux.tile([P, half], F32, name="ss_last", tag="aux")
-            nc.tensor.matmul(
-                out=ss[:], lhsT=ones_f32[:], rhs=sqs[(g, 0)][:, c * half : (c + 1) * half], start=True, stop=False
-            )
-            last_ss.append(ss)
-        for c in range(2):
-            square(g, 1, slice(c * half, (c + 1) * half))
-        scale_store(G - 2, 0)
-        scale_store(G - 2, 1)
-        rinv = work.tile([P, GC], F32, name="rinv")
-        for c in range(2):
-            cs = slice(c * half, (c + 1) * half)
-            nc.tensor.matmul(out=last_ss[c][:], lhsT=ones_f32[:], rhs=sqs[(g, 1)][:, cs], start=False, stop=True)
-            nc.scalar.activation(out=rinv[:, cs], in_=last_ss[c][:], func=ACT.Abs_reciprocal_sqrt)
-        for c in range(2):
-            cs = slice(c * half, (c + 1) * half)
-            o = outp.tile([P, NB // 2, 2, T - 1], F32, name="o_last")
-            for h in range(2):
-                nc.vector.scalar_tensor_tensor(
-                    out=o[:, :, h, :],
-                    in0=rinv[:, cs].rearrange("f (n p) -> f n p", p=T)[:, :, 0 : T - 1],
-                    scalar=1.0e12,
-                    in1=codes[(g, h)][:, cs].rearrange("f (n p) -> f n p", p=T)[:, :, 0 : T - 1],
-                    op0=ALU.min,
-                    op1=ALU.mult,
-                )
-            n0 = g * NB + c * (NB // 2)
-            queue = nc.sync if c == 0 else nc.scalar
-            queue.dma_start(
-                out=out[n0 : n0 + NB // 2].rearrange("n (m h) p -> m n (h p)", h=2),
-                in_=o[:].rearrange("m n h p -> m n (h p)"),
-            )
+        g = LAST
+        passes(g, 0, 4, 0)
+        rsqrt(g - 2)
+        scale(g - 2, 0)
+        scale(g - 2, 1)
+        relu4(g, 0, 0)
+        square(g - 1, 1)
+        split_sum(g - 1)
+        passes(g, 0, 3, 0)
+        merge(g, 0, 3, 0)
+        passes(g, 0, 2, 0)
+        clear(g, 0, 3, 0)
+        merge(g, 0, 2, 0)
+        passes(g, 1, 4, 0)
+        relu4(g, 1, 0)
+        square(g, 0, 0)
+        passes(g, 1, 3, 0)
+        merge(g, 1, 3, 0)
+        passes(g, 1, 2, 0)
+        clear(g, 1, 3, 0)
+        merge(g, 1, 2, 0)
+        passes(g, 0, 4, 1)
+        relu4(g, 0, 1)
+        square(g, 1, 0)
+        split_sum(g, 0)
+        passes(g, 0, 3, 1)
+        merge(g, 0, 3, 1)
+        passes(g, 0, 2, 1)
+        clear(g, 0, 3, 1)
+        merge(g, 0, 2, 1)
+        passes(g, 1, 4, 1)
+        relu4(g, 1, 1)
+        square(g, 0, 1)
+        passes(g, 1, 3, 1)
+        merge(g, 1, 3, 1)
+        sum_filters(g - 1)
+        passes(g, 1, 2, 1)
+        sum_f32(g, 0, 1)
+        clear(g, 1, 3, 1)
+        merge(g, 1, 2, 1)
+        rsqrt(g - 1)
+        square(g, 1, 1)
+        sum_filters(g, 0)
+        sum_f32(g, 1, 1)
+        rsqrt(g, 0)
+        scale(g - 1, 0)
+        scale(g - 1, 1)
+        scale(g, 0, 0)
+        scale(g, 1, 0)
+        rsqrt(g, 1)
+        scale(g, 0, 1)
+        scale(g, 1, 1)

@@ -18,8 +18,7 @@ WIDTHS = (4, 3, 2)
 NB = 4
 G = B // NB
 LAST = G - 1
-L = 4
-PH = T // L
+BLK = 64
 UNIT0 = {4: 0, 3: 4, 2: 7}
 BIAS_COL = {4: 0, 3: 2, 2: 4}
 NCOL = 1024
@@ -51,15 +50,14 @@ def tile_textheading_pa_t_kernel(tc, words_emb, W2, b2, W3, b3, W4, b4, out):
                 out=bias_words[row : row + 1, :], in_=b_dram[K].bitcast(F32).rearrange("(o m) -> o m", o=1)
             )
         x_raw = {}
-        w_raw = {}
         w_tile = {}
 
         def load_x(g, pieces=1):
-            t = raw.tile([P, L, D], BF16, name="x_raw%d" % g)
-            src = words_emb[g * NB : (g + 1) * NB].rearrange("n (ph l) d -> (n ph) l d", l=L)
-            step = L // pieces
-            for l in range(0, L, step):
-                nc.sync.dma_start(out=t[:, l : l + step, :], in_=src[:, l : l + step, :])
+            t = raw.tile([P, NB, D], BF16, name="x_raw%d" % g)
+            src = words_emb[g * NB : (g + 1) * NB].rearrange("n p d -> p n d")
+            step = NB // pieces
+            for n in range(0, NB, step):
+                nc.sync.dma_start(out=t[:, n : n + step, :], in_=src[:, n : n + step, :])
             x_raw[g] = t
 
         def load_w(K, h, k0, cnt):
@@ -69,7 +67,6 @@ def tile_textheading_pa_t_kernel(tc, words_emb, W2, b2, W3, b3, W4, b4, out):
                 out=t[:].rearrange("m (k d) -> m k d", k=cnt), in_=src[:, k0 : k0 + cnt, :]
             )
             for k in range(cnt):
-                w_raw[(K, h, k0 + k)] = t[:, k * D : (k + 1) * D]
                 w_tile[(K, h, k0 + k)] = t[:, k * D : cnt * D]
 
         load_x(0, pieces=2)
@@ -92,6 +89,13 @@ def tile_textheading_pa_t_kernel(tc, words_emb, W2, b2, W3, b3, W4, b4, out):
         nc.scalar.activation(out=dummy[:], in_=one_col[:], func=ACT.Abs_reciprocal_sqrt)
         ident = const.tile([P, P], F32, name="ident")
         make_identity(nc, ident[:])
+        perms = {}
+        for L in (8, 4):
+            perms[L] = const.tile([P, P], F32, name="perm%d" % L)
+            nc.vector.tensor_copy(
+                out=perms[L][:].rearrange("i (pl ph) -> i pl ph", pl=L),
+                in_=ident[:].rearrange("i (ph pl) -> i pl ph", pl=L),
+            )
         zeros = const.tile([P, NB * 3], F32, name="zeros")
         nc.vector.memset(zeros[:], 0.0)
         ones_bf = const.tile([P, P], BF16, name="ones_bf")
@@ -135,7 +139,7 @@ def tile_textheading_pa_t_kernel(tc, words_emb, W2, b2, W3, b3, W4, b4, out):
             grp_w = w_grp[(K, h)][:].bitcast(F32).rearrange("q (c f u) -> q c f u", c=K, f=P, u=2)
             ps = mxp.tile([P, 4, P], F32, name="ps_w", tag="acc")
             for i in range(cnt):
-                words = w_raw[(K, h, k0 + i)].bitcast(F32)
+                words = w_tile[(K, h, k0 + i)][:, 0:D].bitcast(F32)
                 for u in range(2):
                     if (K, h, k0 + i) in w_ord:
                         src = w_ord[(K, h, k0 + i)][:, u, :]
@@ -157,94 +161,79 @@ def tile_textheading_pa_t_kernel(tc, words_emb, W2, b2, W3, b3, W4, b4, out):
                 in_=w_grp[(K, h)][:, k0 * D : (k0 + cnt) * D],
             )
 
+        def parts(g):
+            if g < LAST:
+                return ((g * NB, NB, 0, 8),)
+            return ((g * NB, NB // 2, 0, 4), (g * NB + NB // 2, NB // 2, 512, 4))
+
         ps_x = {}
         x_grp = {}
         x_ord = {}
 
-        def order_x(g, half):
+        def order_x(g, half, eng="s"):
             if half == 0:
-                x_ord[g] = xg.tile([P, L, 2, P], F32, name="x_ord")
-            ls = slice(2 * half, 2 * half + 2)
-            words = x_raw[g][:].rearrange("m l d -> m (l d)").bitcast(F32).rearrange("m (l q u) -> m l u q", l=L, u=2)
-            nc.scalar.copy(out=x_ord[g][:, ls], in_=words[:, ls])
+                x_ord[g] = xg.tile([P, NB, 2, P], F32, name="x_ord")
+            ns = slice(2 * half, 2 * half + 2)
+            src = x_raw[g][:].rearrange("p n d -> p (n d)").bitcast(F32).rearrange("p (n q u) -> p n u q", n=NB, u=2)
+            if eng == "s":
+                nc.scalar.copy(out=x_ord[g][:, ns], in_=src[:, ns])
+            else:
+                nc.vector.tensor_copy(out=x_ord[g][:, ns], in_=src[:, ns])
 
-        def transposes_x(g, parts=(0, 1)):
+        def transposes_x(g, halves=(0, 1)):
             banks = ps_x.setdefault(g, [])
-            for i in parts:
+            perm = perms[parts(g)[0][3]]
+            for i in halves:
                 ps = aux.tile([P, 4, P], F32, name="ps_x", tag="aux")
                 for c in range(2):
                     words = x_raw[g][:, 2 * i + c, :].bitcast(F32)
                     for u in range(2):
                         src = x_ord[g][:, 2 * i + c, u, :] if g in x_ord else words[:, u : 256 : 2]
-                        nc.tensor.transpose(ps[:, 2 * c + u, :], src, ident[:])
+                        nc.tensor.transpose(ps[:, 2 * c + u, :], src, perm[:])
                 banks.append(ps)
 
-        def subs(g):
-            if g < LAST:
-                return ((g * NB, NB, 0, P),)
-            return ((g * NB, NB // 2, 0, P // 2), (g * NB + NB // 2, NB // 2, 512, P // 2))
-
-        def evac_x(g, engines="ss", parts=(0, 1)):
+        def evac_x(g, n, eng):
             if g not in x_grp:
                 x_grp[g] = xg.tile([P, 512 * 4], BF16, name="x_grp", align_bytes=64)
-            grp = x_grp[g]
-            ns = len(subs(g))
-            dst = grp[:].bitcast(F32).rearrange("q (s l m u) -> q s l m u", s=ns, l=L, u=2)
-            for i in parts:
-                src = ps_x[g][i][:].rearrange("q (c u) (s m) -> q s c m u", u=2, s=ns)
-                for s in range(ns):
-                    if engines[i] == "v":
-                        nc.vector.tensor_copy(out=dst[:, s, 2 * i : 2 * i + 2], in_=src[:, s])
-                    else:
-                        nc.scalar.copy(out=dst[:, s, 2 * i : 2 * i + 2], in_=src[:, s])
-
-        def quant_half(g, i):
-            codes, scales = planes[g % 3]
-            cols = slice(i * 256, (i + 1) * 256)
-            nc.vector.quantize_mx(
-                out=codes[:, cols].bitcast(FP8X4), scales=scales[:, cols], in_=x_grp[g][:, i * 1024 : (i + 1) * 1024]
-            )
+            n0, nb, c0, L = parts(g)[n * len(parts(g)) // NB]
+            grp = x_grp[g][:, c0 * 2 : c0 * 2 + L * BLK * 4].bitcast(F32)
+            dst = grp.rearrange("q (l n ph u) -> q l n ph u", l=L, n=nb, u=2)[:, :, n % nb]
+            src = ps_x[g][n // 2][:, 2 * (n % 2) : 2 * (n % 2) + 2, :].rearrange("q u (l ph) -> q l ph u", l=L)
+            if eng == "v":
+                nc.vector.tensor_copy(out=dst, in_=src)
+            else:
+                nc.scalar.copy(out=dst, in_=src)
 
         def quant_x(g):
             codes, scales = planes[g % 3]
-            for s, (n0, nb, c0, blk) in enumerate(subs(g)):
-                w = L * blk
+            for n0, nb, c0, L in parts(g):
+                w = L * BLK
                 nc.vector.quantize_mx(
                     out=codes[:, c0 : c0 + w].bitcast(FP8X4),
                     scales=scales[:, c0 : c0 + w],
-                    in_=x_grp[g][:, s * w * 4 : (s + 1) * w * 4],
+                    in_=x_grp[g][:, c0 * 2 : c0 * 2 + w * 4],
                 )
-
-        def halo_codes(g):
-            codes = planes[g % 3][0]
-            for n0, nb, c0, blk in subs(g):
-                w = L * blk
-                r = 3 * blk
-                nc.vector.tensor_copy(
-                    out=codes[:, c0 + w : c0 + w + r].bitcast(I32), in_=codes[:, c0 + 1 : c0 + 1 + r].bitcast(I32)
-                )
-
-        def halo_scales(g):
-            scales = planes[g % 3][1]
-            for n0, nb, c0, blk in subs(g):
-                w = L * blk
-                r = 3 * blk
-                nc.vector.tensor_copy(out=scales[:, c0 + w : c0 + w + r], in_=scales[:, c0 + 1 : c0 + 1 + r])
 
         def halo(g):
-            halo_codes(g)
-            halo_scales(g)
+            codes, scales = planes[g % 3]
+            r = 3 * BLK
+            for n0, nb, c0, L in parts(g):
+                w = c0 + L * BLK
+                nc.vector.tensor_copy(
+                    out=codes[:, w : w + r].bitcast(I32), in_=codes[:, c0 + 1 : c0 + 1 + r].bitcast(I32)
+                )
+                nc.vector.tensor_copy(out=scales[:, w : w + r], in_=scales[:, c0 + 1 : c0 + 1 + r])
 
         accs = {}
         code_of = {}
 
         def passes(g, h, K, s=0):
-            n0, nb, c0, blk = subs(g)[s]
+            n0, nb, c0, L = parts(g)[s]
             codes, scales = planes[g % 3]
-            acc = mxp.tile([P, L * blk], F32, name="acc", tag="acc")
+            acc = mxp.tile([P, L * BLK], F32, name="acc", tag="acc")
             for k in range(K):
                 unit = h * 9 + UNIT0[K] + k
-                cols = slice(c0 + k * blk, c0 + (k + L) * blk)
+                cols = slice(c0 + k * BLK, c0 + (k + L) * BLK)
                 nc.tensor.matmul_mx(
                     out=acc[:],
                     lhsT=w_codes[:, unit * P : (unit + 1) * P].bitcast(FP8X4),
@@ -257,80 +246,81 @@ def tile_textheading_pa_t_kernel(tc, words_emb, W2, b2, W3, b3, W4, b4, out):
             accs[(g, h, K, s)] = acc
 
         def relu4(g, h, s=0):
-            n0, nb, c0, blk = subs(g)[s]
+            n0, nb, c0, L = parts(g)[s]
             code = code_pool.tile([P, nb * T], F32, name="code%d" % h)
             code_of[(g, h, s)] = code
             nc.scalar.activation(
-                out=code[:].rearrange("f (m l) -> f m l", l=L),
-                in_=accs[(g, h, 4, s)][:].rearrange("f (l m) -> f m l", l=L),
+                out=code[:].rearrange("f (m a b) -> f a m b", a=L // 4, b=4),
+                in_=accs[(g, h, 4, s)][:].rearrange("f (a b m) -> f a m b", a=L // 4, b=4),
                 func=ACT.Relu,
                 bias=bias_sb[:, BIAS_COL[4] + h : BIAS_COL[4] + h + 1],
             )
-            clear(g, h, 4, s)
-
-        def clear(g, h, K, s=0):
-            nb = subs(g)[s][1]
-            last = code_of[(g, h, s)][:].rearrange("f (n p) -> f n p", p=T)[:, :, T - K + 1 : T]
-            if K == 4:
-                nc.scalar.copy(out=last, in_=zeros[:, 0 : nb * (K - 1)].rearrange("f (n p) -> f n p", p=K - 1))
-            else:
-                nc.vector.memset(last, 0.0)
-
-        def merge(g, h, K, s=0):
-            code_v = code_of[(g, h, s)][:].rearrange("f (m l) -> f m l", l=L)
-            nc.vector.scalar_tensor_tensor(
-                out=code_v,
-                in0=accs[(g, h, K, s)][:].rearrange("f (l m) -> f m l", l=L),
-                scalar=bias_sb[:, BIAS_COL[K] + h : BIAS_COL[K] + h + 1],
-                in1=code_v,
-                op0=ALU.add,
-                op1=ALU.max,
+            nc.scalar.copy(
+                out=code[:].rearrange("f (n p) -> f n p", p=T)[:, :, T - 3 : T],
+                in_=zeros[:, 0 : nb * 3].rearrange("f (n p) -> f n p", p=3),
             )
 
+        def merge(g, h, K, s=0):
+            n0, nb, c0, L = parts(g)[s]
+            code = code_of[(g, h, s)]
+            code_v = code[:].rearrange("f (m l) -> f m l", l=L)
+            acc_v = accs[(g, h, K, s)][:].rearrange("f (l m) -> f m l", l=L)
+            for a in range(0, L, 4):
+                nc.vector.scalar_tensor_tensor(
+                    out=code_v[:, :, a : a + 4],
+                    in0=acc_v[:, :, a : a + 4],
+                    scalar=bias_sb[:, BIAS_COL[K] + h : BIAS_COL[K] + h + 1],
+                    in1=code_v[:, :, a : a + 4],
+                    op0=ALU.add,
+                    op1=ALU.max,
+                )
+            if K == 3:
+                nc.vector.memset(code[:].rearrange("f (n p) -> f n p", p=T)[:, :, T - 2 : T], 0.0)
+
         sqs = {}
-        tots = {}
         his = {}
         los = {}
         rinvs = {}
         sss = {}
         outs = {}
 
-        def cols_of(g, s):
-            return subs(g)[s][1] * T
+        def width(g, s):
+            return parts(g)[s][1] * T
 
         def square(g, h, s=0):
-            sqs[(g, h, s)] = work.tile([P, cols_of(g, s)], F32, name="sq%d" % h)
+            sqs[(g, h, s)] = work.tile([P, width(g, s)], F32, name="sq%d" % h)
             nc.scalar.activation(out=sqs[(g, h, s)][:], in_=code_of[(g, h, s)][:], func=ACT.Square)
 
-        def split_sum(g, s=0):
-            tot = work.tile([P, cols_of(g, s)], F32, name="tot")
-            nc.gpsimd.tensor_tensor(out=tot[:], in0=sqs[(g, 0, s)][:], in1=sqs[(g, 1, s)][:], op=ALU.add)
-            hi = split.tile([P, cols_of(g, s)], BF16, name="hi")
+        def split_sum(g, s=0, adder="p"):
+            tot = work.tile([P, width(g, s)], F32, name="tot")
+            eng = nc.gpsimd if adder == "p" else nc.vector
+            eng.tensor_tensor(out=tot[:], in0=sqs[(g, 0, s)][:], in1=sqs[(g, 1, s)][:], op=ALU.add)
+            hi = split.tile([P, width(g, s)], BF16, name="hi")
             nc.gpsimd.tensor_scalar(out=hi[:], in0=tot[:], scalar1=1.0, scalar2=0.0, op0=ALU.mult, op1=ALU.add)
-            lo = split.tile([P, cols_of(g, s)], BF16, name="lo")
+            lo = split.tile([P, width(g, s)], BF16, name="lo")
             nc.gpsimd.tensor_tensor(out=lo[:], in0=tot[:], in1=hi[:], op=ALU.subtract)
             his[(g, s)] = hi
             los[(g, s)] = lo
 
         def sum_filters(g, s=0):
-            ss = aux.tile([P, cols_of(g, s)], F32, name="ss", tag="aux")
+            ss = aux.tile([P, width(g, s)], F32, name="ss", tag="aux")
             nc.tensor.matmul(out=ss[:], lhsT=ones_bf[:], rhs=his[(g, s)][:], start=True, stop=False)
             nc.tensor.matmul(out=ss[:], lhsT=ones_bf[:], rhs=los[(g, s)][:], start=False, stop=True)
             sss[(g, s)] = ss
 
         def sum_f32(g, h, s):
             if h == 0:
-                sss[(g, s)] = aux.tile([P, cols_of(g, s)], F32, name="ss", tag="aux")
+                sss[(g, s)] = aux.tile([P, width(g, s)], F32, name="ss", tag="aux")
             nc.tensor.matmul(
                 out=sss[(g, s)][:], lhsT=ones_f32[:], rhs=sqs[(g, h, s)][:], start=(h == 0), stop=(h == 1)
             )
 
         def rsqrt(g, s=0):
-            rinvs[(g, s)] = work.tile([P, cols_of(g, s)], F32, name="rinv")
+            rinvs[(g, s)] = work.tile([P, width(g, s)], F32, name="rinv")
             nc.scalar.activation(out=rinvs[(g, s)][:], in_=sss[(g, s)][:], func=ACT.Abs_reciprocal_sqrt)
 
         def scale(g, h, s=0):
-            n0, nb, c0, blk = subs(g)[s]
+            n0, nb, c0, L = parts(g)[s]
             if h == 0:
                 outs[(g, s)] = outp.tile([P, nb, 2, T - 1], F32, name="o")
             nc.vector.scalar_tensor_tensor(
@@ -347,14 +337,19 @@ def tile_textheading_pa_t_kernel(tc, words_emb, W2, b2, W3, b3, W4, b4, out):
                     in_=outs[(g, s)][:].rearrange("m n h p -> m n (h p)"),
                 )
 
+        def evac4(g, engines):
+            for n in range(NB):
+                evac_x(g, n, engines[n])
+
         warm_up(WARM)
         transposes_x(0, (0,))
-        evac_x(0, "ss", (0,))
+        evac_x(0, 0, "s")
+        evac_x(0, 1, "v")
         transposes_x(0, (1,))
-        evac_x(0, "vv", (1,))
-        quant_half(0, 0)
+        evac_x(0, 2, "s")
+        evac_x(0, 3, "v")
         trans_w(4, 0, 0, 2, "s")
-        quant_half(0, 1)
+        quant_x(0)
         trans_w(4, 0, 2, 2, "s")
         quant_w(4, 0, 0, 2)
         halo(0)
@@ -378,7 +373,7 @@ def tile_textheading_pa_t_kernel(tc, words_emb, W2, b2, W3, b3, W4, b4, out):
         order_w(3, 1, 0, 2)
         relu4(0, 0)
         transposes_x(1)
-        evac_x(1, "sv")
+        evac4(1, "svsv")
         passes(0, 0, 3)
         quant_x(1)
         passes(0, 0, 2)
@@ -387,7 +382,6 @@ def tile_textheading_pa_t_kernel(tc, words_emb, W2, b2, W3, b3, W4, b4, out):
         halo(1)
         trans_w(4, 1, 0, 2, "s")
         trans_w(4, 1, 2, 2, "s")
-        clear(0, 0, 3)
         merge(0, 0, 2)
         quant_w(4, 1, 0, 4)
         passes(1, 0, 4)
@@ -403,98 +397,89 @@ def tile_textheading_pa_t_kernel(tc, words_emb, W2, b2, W3, b3, W4, b4, out):
         square(0, 0)
         passes(1, 0, 2)
         quant_w(2, 1, 0, 2)
-        clear(1, 0, 3)
         merge(1, 0, 2)
-        passes(0, 1, 4)
         order_x(2, 1)
+        passes(0, 1, 4)
+        transposes_x(2)
         relu4(0, 1)
+        evac4(2, "svsv")
         order_x(3, 0)
         passes(0, 1, 3)
         merge(0, 1, 3)
-        passes(0, 1, 2)
-        transposes_x(2)
-        clear(0, 1, 3)
-        merge(0, 1, 2)
-        order_x(3, 1)
-        evac_x(2, "sv")
-        passes(1, 1, 4)
         quant_x(2)
+        passes(0, 1, 2)
+        merge(0, 1, 2)
+        halo(2)
+        order_x(3, 1)
+        square(1, 0)
+        passes(1, 1, 4)
+        transposes_x(3)
         relu4(1, 1)
         square(0, 1)
         split_sum(0)
-        passes(1, 1, 3)
-        merge(1, 1, 3)
-        halo(2)
-        square(1, 0)
-        passes(1, 1, 2)
-        clear(1, 1, 3)
-        merge(1, 1, 2)
         order_x(4, 0)
         order_x(4, 1)
-        transposes_x(3)
+        passes(1, 1, 3)
+        merge(1, 1, 3)
+        evac4(3, "svsv")
+        passes(1, 1, 2)
+        merge(1, 1, 2)
+        transposes_x(4)
 
         for g in range(2, LAST):
             passes(g, 0, 4)
-            evac_x(g + 1, "ss", (0,))
-            evac_x(g + 1, "vv", (1,))
-            if g > 2:
-                rsqrt(g - 2)
             quant_x(g + 1)
+            if g + 3 < G:
+                order_x(g + 3, 0)
             if g > 2:
-                scale(g - 2, 0)
-                scale(g - 2, 1)
+                scale(g - 3, 0)
+                scale(g - 3, 1)
+            halo(g + 1)
             relu4(g, 0)
             square(g - 1, 1)
             split_sum(g - 1)
             passes(g, 0, 3)
             merge(g, 0, 3)
-            halo_scales(g + 1)
-            passes(g, 0, 2)
-            clear(g, 0, 3)
-            merge(g, 0, 2)
-            if g == 2:
-                sum_filters(0)
-                rsqrt(0)
-                scale(0, 0)
-                scale(0, 1)
             if g + 3 < G:
-                order_x(g + 3, 0)
+                order_x(g + 3, 1)
+            passes(g, 0, 2)
+            merge(g, 0, 2)
+            sum_filters(g - 2)
+            rsqrt(g - 2)
+            if g + 2 < G:
+                evac4(g + 2, "ssvv")
             passes(g, 1, 4)
             relu4(g, 1)
             square(g, 0)
             passes(g, 1, 3)
             merge(g, 1, 3)
-            halo_codes(g + 1)
-            if g + 3 < G:
-                order_x(g + 3, 1)
             passes(g, 1, 2)
-            clear(g, 1, 3)
             merge(g, 1, 2)
-            if g + 2 < G:
-                transposes_x(g + 2)
-            sum_filters(g - 1)
+            if g == LAST - 1:
+                scale(g - 2, 0)
+            if g + 3 < G:
+                transposes_x(g + 3)
 
         g = LAST
         passes(g, 0, 4, 0)
-        rsqrt(g - 2)
-        scale(g - 2, 0)
-        scale(g - 2, 1)
-        relu4(g, 0, 0)
         square(g - 1, 1)
-        split_sum(g - 1)
+        relu4(g, 0, 0)
         passes(g, 0, 3, 0)
         merge(g, 0, 3, 0)
+        split_sum(g - 1, adder="v")
         passes(g, 0, 2, 0)
-        clear(g, 0, 3, 0)
         merge(g, 0, 2, 0)
+        scale(g - 3, 1)
+        sum_filters(g - 2)
+        rsqrt(g - 2)
         passes(g, 1, 4, 0)
         relu4(g, 1, 0)
         square(g, 0, 0)
         passes(g, 1, 3, 0)
         merge(g, 1, 3, 0)
         passes(g, 1, 2, 0)
-        clear(g, 1, 3, 0)
         merge(g, 1, 2, 0)
+        scale(g - 2, 0)
         passes(g, 0, 4, 1)
         relu4(g, 0, 1)
         square(g, 1, 0)
@@ -502,20 +487,19 @@ def tile_textheading_pa_t_kernel(tc, words_emb, W2, b2, W3, b3, W4, b4, out):
         passes(g, 0, 3, 1)
         merge(g, 0, 3, 1)
         passes(g, 0, 2, 1)
-        clear(g, 0, 3, 1)
         merge(g, 0, 2, 1)
+        scale(g - 2, 1)
         passes(g, 1, 4, 1)
         relu4(g, 1, 1)
         square(g, 0, 1)
         passes(g, 1, 3, 1)
         merge(g, 1, 3, 1)
-        sum_filters(g - 1)
         passes(g, 1, 2, 1)
+        sum_filters(g - 1)
         sum_f32(g, 0, 1)
-        clear(g, 1, 3, 1)
         merge(g, 1, 2, 1)
-        rsqrt(g - 1)
         square(g, 1, 1)
+        rsqrt(g - 1)
         sum_filters(g, 0)
         sum_f32(g, 1, 1)
         rsqrt(g, 0)

@@ -121,18 +121,6 @@ def tile_textheading_pa_t_kernel(tc, words_emb, W2, b2, W3, b3, W4, b4, out):
                 nc.tensor.matmul(out=ps_warm[:], lhsT=warm[:, 0:P], rhs=warm[:], start=True, stop=True)
 
         w_grp = {}
-        w_ord = {}
-
-        def order_w(K, h, k0, cnt, eng="s"):
-            t = raw.tile([P, cnt, 2, P], F32, name="w_ord%d_%d_%d" % (K, h, k0))
-            for k in range(cnt):
-                w_ord[(K, h, k0 + k)] = t[:, k]
-            src = w_tile[(K, h, k0)][:, 0 : cnt * D].bitcast(F32).rearrange("m (k q u) -> m k u q", k=cnt, u=2)
-            if eng == "s":
-                nc.scalar.copy(out=t[:], in_=src)
-            else:
-                nc.vector.tensor_copy(out=t[:], in_=src)
-
         def trans_w(K, h, k0, cnt, eng):
             if (K, h) not in w_grp:
                 w_grp[(K, h)] = raw.tile([P, K * D], BF16, name="w_grp%d_%d" % (K, h), align_bytes=64)
@@ -141,11 +129,7 @@ def tile_textheading_pa_t_kernel(tc, words_emb, W2, b2, W3, b3, W4, b4, out):
             for i in range(cnt):
                 words = w_tile[(K, h, k0 + i)][:, 0:D].bitcast(F32)
                 for u in range(2):
-                    if (K, h, k0 + i) in w_ord:
-                        src = w_ord[(K, h, k0 + i)][:, u, :]
-                    else:
-                        src = words[:, u : 256 : 2]
-                    nc.tensor.transpose(ps[:, 2 * i + u, :], src, ident[:])
+                    nc.tensor.transpose(ps[:, 2 * i + u, :], words[:, u : 256 : 2], ident[:])
             src = ps[:, 0 : 2 * cnt, :].rearrange("q (c u) f -> q c f u", u=2)
             if eng == "s":
                 nc.scalar.copy(out=grp_w[:, k0 : k0 + cnt], in_=src)
@@ -162,23 +146,10 @@ def tile_textheading_pa_t_kernel(tc, words_emb, W2, b2, W3, b3, W4, b4, out):
             )
 
         def parts(g):
-            if g < LAST:
-                return ((g * NB, NB, 0, 8),)
-            return ((g * NB, NB // 2, 0, 4), (g * NB + NB // 2, NB // 2, 512, 4))
+            return ((g * NB, NB, 0, 8),)
 
         ps_x = {}
         x_grp = {}
-        x_ord = {}
-
-        def order_x(g, half, eng="s"):
-            if half == 0:
-                x_ord[g] = xg.tile([P, NB, 2, P], F32, name="x_ord")
-            ns = slice(2 * half, 2 * half + 2)
-            src = x_raw[g][:].rearrange("p n d -> p (n d)").bitcast(F32).rearrange("p (n q u) -> p n u q", n=NB, u=2)
-            if eng == "s":
-                nc.scalar.copy(out=x_ord[g][:, ns], in_=src[:, ns])
-            else:
-                nc.vector.tensor_copy(out=x_ord[g][:, ns], in_=src[:, ns])
 
         def transposes_x(g, halves=(0, 1)):
             banks = ps_x.setdefault(g, [])
@@ -188,8 +159,7 @@ def tile_textheading_pa_t_kernel(tc, words_emb, W2, b2, W3, b3, W4, b4, out):
                 for c in range(2):
                     words = x_raw[g][:, 2 * i + c, :].bitcast(F32)
                     for u in range(2):
-                        src = x_ord[g][:, 2 * i + c, u, :] if g in x_ord else words[:, u : 256 : 2]
-                        nc.tensor.transpose(ps[:, 2 * c + u, :], src, perm[:])
+                        nc.tensor.transpose(ps[:, 2 * c + u, :], words[:, u : 256 : 2], perm[:])
                 banks.append(ps)
 
         def evac_x(g, n, eng):
@@ -260,22 +230,20 @@ def tile_textheading_pa_t_kernel(tc, words_emb, W2, b2, W3, b3, W4, b4, out):
                 in_=zeros[:, 0 : nb * 3].rearrange("f (n p) -> f n p", p=3),
             )
 
-        def merge(g, h, K, s=0):
+        def merge(g, h, K, ns=slice(0, NB), s=0):
             n0, nb, c0, L = parts(g)[s]
-            code = code_of[(g, h, s)]
-            code_v = code[:].rearrange("f (m l) -> f m l", l=L)
+            ms = slice(ns.start * T // L, ns.stop * T // L)
+            code_v = code_of[(g, h, s)][:].rearrange("f (m l) -> f m l", l=L)
             acc_v = accs[(g, h, K, s)][:].rearrange("f (l m) -> f m l", l=L)
             for a in range(0, L, 4):
                 nc.vector.scalar_tensor_tensor(
-                    out=code_v[:, :, a : a + 4],
-                    in0=acc_v[:, :, a : a + 4],
+                    out=code_v[:, ms, a : a + 4],
+                    in0=acc_v[:, ms, a : a + 4],
                     scalar=bias_sb[:, BIAS_COL[K] + h : BIAS_COL[K] + h + 1],
-                    in1=code_v[:, :, a : a + 4],
+                    in1=code_v[:, ms, a : a + 4],
                     op0=ALU.add,
                     op1=ALU.max,
                 )
-            if K == 3:
-                nc.vector.memset(code[:].rearrange("f (n p) -> f n p", p=T)[:, :, T - 2 : T], 0.0)
 
         sqs = {}
         his = {}
@@ -287,33 +255,50 @@ def tile_textheading_pa_t_kernel(tc, words_emb, W2, b2, W3, b3, W4, b4, out):
         def width(g, s):
             return parts(g)[s][1] * T
 
-        def square(g, h, s=0):
-            sqs[(g, h, s)] = work.tile([P, width(g, s)], F32, name="sq%d" % h)
-            nc.scalar.activation(out=sqs[(g, h, s)][:], in_=code_of[(g, h, s)][:], func=ACT.Square)
+        def square(g, h, ns=slice(0, NB), s=0):
+            n0, nb, c0, L = parts(g)[s]
+            nc.scalar.activation(
+                out=code_of[(g, h, s)][:].rearrange("f (n p) -> f n p", p=T)[:, ns, T - 2],
+                in_=accs[(g, h, 2, s)][:].rearrange("f (l n ph) -> f l n ph", l=L, n=nb)[:, L - 2, ns, T // L - 1],
+                func=ACT.Relu,
+                bias=bias_sb[:, BIAS_COL[2] + h : BIAS_COL[2] + h + 1],
+            )
+            if (g, h, s) not in sqs:
+                sqs[(g, h, s)] = work.tile([P, width(g, s)], F32, name="sq%d" % h)
+            cs = slice(ns.start * T, ns.stop * T)
+            nc.scalar.activation(out=sqs[(g, h, s)][:, cs], in_=code_of[(g, h, s)][:, cs], func=ACT.Square)
 
-        def split_sum(g, s=0, adder="p"):
-            tot = work.tile([P, width(g, s)], F32, name="tot")
-            eng = nc.gpsimd if adder == "p" else nc.vector
-            eng.tensor_tensor(out=tot[:], in0=sqs[(g, 0, s)][:], in1=sqs[(g, 1, s)][:], op=ALU.add)
-            hi = split.tile([P, width(g, s)], BF16, name="hi")
-            nc.gpsimd.tensor_scalar(out=hi[:], in0=tot[:], scalar1=1.0, scalar2=0.0, op0=ALU.mult, op1=ALU.add)
-            lo = split.tile([P, width(g, s)], BF16, name="lo")
-            nc.gpsimd.tensor_tensor(out=lo[:], in0=tot[:], in1=hi[:], op=ALU.subtract)
-            his[(g, s)] = hi
-            los[(g, s)] = lo
+        tots = {}
+
+        def add_halves(g, s=0, eng="p"):
+            tots[(g, s)] = work.tile([P, width(g, s)], F32, name="tot")
+            e = nc.gpsimd if eng == "p" else nc.vector
+            e.tensor_tensor(out=tots[(g, s)][:], in0=sqs[(g, 0, s)][:], in1=sqs[(g, 1, s)][:], op=ALU.add)
+
+        def high_part(g, s=0, eng="p"):
+            his[(g, s)] = split.tile([P, width(g, s)], BF16, name="hi")
+            if eng == "p":
+                nc.gpsimd.tensor_scalar(
+                    out=his[(g, s)][:], in0=tots[(g, s)][:], scalar1=1.0, scalar2=0.0, op0=ALU.mult, op1=ALU.add
+                )
+            else:
+                nc.scalar.copy(out=his[(g, s)][:], in_=tots[(g, s)][:])
+
+        def low_part(g, s=0, eng="p"):
+            los[(g, s)] = split.tile([P, width(g, s)], BF16, name="lo")
+            e = nc.gpsimd if eng == "p" else nc.vector
+            e.tensor_tensor(out=los[(g, s)][:], in0=tots[(g, s)][:], in1=his[(g, s)][:], op=ALU.subtract)
+
+        def split_sum(g, s=0):
+            add_halves(g, s)
+            high_part(g, s)
+            low_part(g, s)
 
         def sum_filters(g, s=0):
             ss = aux.tile([P, width(g, s)], F32, name="ss", tag="aux")
             nc.tensor.matmul(out=ss[:], lhsT=ones_bf[:], rhs=his[(g, s)][:], start=True, stop=False)
             nc.tensor.matmul(out=ss[:], lhsT=ones_bf[:], rhs=los[(g, s)][:], start=False, stop=True)
             sss[(g, s)] = ss
-
-        def sum_f32(g, h, s):
-            if h == 0:
-                sss[(g, s)] = aux.tile([P, width(g, s)], F32, name="ss", tag="aux")
-            nc.tensor.matmul(
-                out=sss[(g, s)][:], lhsT=ones_f32[:], rhs=sqs[(g, h, s)][:], start=(h == 0), stop=(h == 1)
-            )
 
         def rsqrt(g, s=0):
             rinvs[(g, s)] = work.tile([P, width(g, s)], F32, name="rinv")
@@ -351,6 +336,7 @@ def tile_textheading_pa_t_kernel(tc, words_emb, W2, b2, W3, b3, W4, b4, out):
         trans_w(4, 0, 0, 2, "s")
         quant_x(0)
         trans_w(4, 0, 2, 2, "s")
+        warm_up(2)
         quant_w(4, 0, 0, 2)
         halo(0)
         quant_w(4, 0, 2, 2)
@@ -364,22 +350,15 @@ def tile_textheading_pa_t_kernel(tc, words_emb, W2, b2, W3, b3, W4, b4, out):
         nc.vector.tensor_copy(out=bias_pairs[:], in_=ps_b[:, 0:3])
         quant_w(2, 0, 0, 2)
         nc.vector.tensor_copy(out=bias_sb[:], in_=bias_pairs[:].bitcast(BF16))
-        order_x(1, 0)
         passes(0, 0, 4)
-        order_x(1, 1)
-        order_w(4, 1, 0, 2, "v")
-        order_w(4, 1, 2, 2, "v")
-        order_w(3, 1, 2, 1, "v")
-        order_w(3, 1, 0, 2)
         relu4(0, 0)
         transposes_x(1)
-        evac4(1, "svsv")
+        evac4(1, "vvvs")
         passes(0, 0, 3)
         quant_x(1)
         passes(0, 0, 2)
-        order_w(2, 1, 0, 2)
-        merge(0, 0, 3)
         halo(1)
+        merge(0, 0, 3)
         trans_w(4, 1, 0, 2, "s")
         trans_w(4, 1, 2, 2, "s")
         merge(0, 0, 2)
@@ -391,122 +370,127 @@ def tile_textheading_pa_t_kernel(tc, words_emb, W2, b2, W3, b3, W4, b4, out):
         quant_w(3, 1, 2, 1)
         quant_w(3, 1, 0, 2)
         passes(1, 0, 3)
-        order_x(2, 0)
         merge(1, 0, 3)
         trans_w(2, 1, 0, 2, "s")
         square(0, 0)
         passes(1, 0, 2)
         quant_w(2, 1, 0, 2)
         merge(1, 0, 2)
-        order_x(2, 1)
         passes(0, 1, 4)
         transposes_x(2)
         relu4(0, 1)
         evac4(2, "svsv")
-        order_x(3, 0)
         passes(0, 1, 3)
         merge(0, 1, 3)
         quant_x(2)
         passes(0, 1, 2)
         merge(0, 1, 2)
         halo(2)
-        order_x(3, 1)
         square(1, 0)
         passes(1, 1, 4)
         transposes_x(3)
         relu4(1, 1)
         square(0, 1)
         split_sum(0)
-        order_x(4, 0)
-        order_x(4, 1)
         passes(1, 1, 3)
-        merge(1, 1, 3)
         evac4(3, "svsv")
+        merge(1, 1, 3)
         passes(1, 1, 2)
         merge(1, 1, 2)
+        quant_x(3)
         transposes_x(4)
 
         for g in range(2, LAST):
             passes(g, 0, 4)
-            quant_x(g + 1)
-            if g + 3 < G:
-                order_x(g + 3, 0)
-            if g > 2:
-                scale(g - 3, 0)
-                scale(g - 3, 1)
             halo(g + 1)
-            relu4(g, 0)
+            if g > 2:
+                rsqrt(g - 2)
+                scale(g - 2, 0)
+                scale(g - 2, 1)
+            if g + 2 < G:
+                evac_x(g + 2, 1, "s")
             square(g - 1, 1)
+            relu4(g, 0)
             split_sum(g - 1)
             passes(g, 0, 3)
             merge(g, 0, 3)
-            if g + 3 < G:
-                order_x(g + 3, 1)
+            if g + 2 < G:
+                evac_x(g + 2, 0, "v")
+                evac_x(g + 2, 2, "s")
+                evac_x(g + 2, 3, "s")
             passes(g, 0, 2)
             merge(g, 0, 2)
-            sum_filters(g - 2)
-            rsqrt(g - 2)
-            if g + 2 < G:
-                evac4(g + 2, "ssvv")
+            if g == 2:
+                sum_filters(0)
+                rsqrt(0)
+                scale(0, 0)
+                scale(0, 1)
             passes(g, 1, 4)
             relu4(g, 1)
             square(g, 0)
             passes(g, 1, 3)
             merge(g, 1, 3)
+            if g + 2 < G:
+                quant_x(g + 2)
             passes(g, 1, 2)
             merge(g, 1, 2)
-            if g == LAST - 1:
-                scale(g - 2, 0)
             if g + 3 < G:
                 transposes_x(g + 3)
+            sum_filters(g - 1)
 
         g = LAST
-        passes(g, 0, 4, 0)
+        halves = (slice(0, 2), slice(2, 4))
+        passes(g, 0, 4)
         square(g - 1, 1)
-        relu4(g, 0, 0)
-        passes(g, 0, 3, 0)
-        merge(g, 0, 3, 0)
-        split_sum(g - 1, adder="v")
-        passes(g, 0, 2, 0)
-        merge(g, 0, 2, 0)
-        scale(g - 3, 1)
-        sum_filters(g - 2)
         rsqrt(g - 2)
-        passes(g, 1, 4, 0)
-        relu4(g, 1, 0)
-        square(g, 0, 0)
-        passes(g, 1, 3, 0)
-        merge(g, 1, 3, 0)
-        passes(g, 1, 2, 0)
-        merge(g, 1, 2, 0)
+        relu4(g, 0)
         scale(g - 2, 0)
-        passes(g, 0, 4, 1)
-        relu4(g, 0, 1)
-        square(g, 1, 0)
-        split_sum(g, 0)
-        passes(g, 0, 3, 1)
-        merge(g, 0, 3, 1)
-        passes(g, 0, 2, 1)
-        merge(g, 0, 2, 1)
         scale(g - 2, 1)
-        passes(g, 1, 4, 1)
-        relu4(g, 1, 1)
-        square(g, 0, 1)
-        passes(g, 1, 3, 1)
-        merge(g, 1, 3, 1)
-        passes(g, 1, 2, 1)
+        split_sum(g - 1)
+        passes(g, 0, 3)
+        merge(g, 0, 3)
+        passes(g, 0, 2)
+        merge(g, 0, 2)
+        passes(g, 1, 4)
+        relu4(g, 1)
+        square(g, 0)
+        passes(g, 1, 3)
+        merge(g, 1, 3)
+        passes(g, 1, 2)
         sum_filters(g - 1)
-        sum_f32(g, 0, 1)
-        merge(g, 1, 2, 1)
-        square(g, 1, 1)
+        last_ss = []
+        for ns in halves:
+            ss = aux.tile([P, 2 * T], F32, name="ss_last", tag="aux")
+            cs = slice(ns.start * T, ns.stop * T)
+            nc.tensor.matmul(out=ss[:], lhsT=ones_f32[:], rhs=sqs[(g, 0, 0)][:, cs], start=True, stop=False)
+            last_ss.append(ss)
+        merge(g, 1, 2, halves[0])
+        square(g, 1, halves[0])
         rsqrt(g - 1)
-        sum_filters(g, 0)
-        sum_f32(g, 1, 1)
-        rsqrt(g, 0)
+        merge(g, 1, 2, halves[1])
+        square(g, 1, halves[1])
         scale(g - 1, 0)
         scale(g - 1, 1)
-        scale(g, 0, 0)
-        scale(g, 1, 0)
-        rsqrt(g, 1)
-        scale(g, 0, 1)
-        scale(g, 1, 1)
+        rinv = work.tile([P, NB * T], F32, name="rinv")
+        for i, ns in enumerate(halves):
+            cs = slice(ns.start * T, ns.stop * T)
+            nc.tensor.matmul(out=last_ss[i][:], lhsT=ones_f32[:], rhs=sqs[(g, 1, 0)][:, cs], start=False, stop=True)
+            nc.scalar.activation(out=rinv[:, cs], in_=last_ss[i][:], func=ACT.Abs_reciprocal_sqrt)
+        for i, ns in enumerate(halves):
+            cs = slice(ns.start * T, ns.stop * T)
+            o = outp.tile([P, NB // 2, 2, T - 1], F32, name="o_last")
+            for h in range(2):
+                nc.vector.scalar_tensor_tensor(
+                    out=o[:, :, h, :],
+                    in0=rinv[:, cs].rearrange("f (n p) -> f n p", p=T)[:, :, 0 : T - 1],
+                    scalar=1.0e12,
+                    in1=code_of[(g, h, 0)][:, cs].rearrange("f (n p) -> f n p", p=T)[:, :, 0 : T - 1],
+                    op0=ALU.min,
+                    op1=ALU.mult,
+                )
+            n0 = g * NB + 2 * i
+            queue = nc.sync if i == 0 else nc.scalar
+            queue.dma_start(
+                out=out[n0 : n0 + 2].rearrange("n (m h) p -> m n (h p)", h=2),
+                in_=o[:].rearrange("m n h p -> m n (h p)"),
+            )

@@ -121,6 +121,20 @@ def tile_textheading_pa_t_kernel(tc, words_emb, W2, b2, W3, b3, W4, b4, out):
                 nc.tensor.matmul(out=ps_warm[:], lhsT=warm[:, 0:P], rhs=warm[:], start=True, stop=True)
 
         w_grp = {}
+        w_ord = {}
+
+        def order_words(out, src, eng):
+            if eng == "s":
+                nc.scalar.copy(out=out, in_=src)
+            else:
+                nc.vector.tensor_copy(out=out, in_=src)
+
+        def order_w(K, h, k0, cnt, eng):
+            t = raw.tile([P, cnt, 2, P], F32, name="w_ord%d_%d_%d" % (K, h, k0))
+            for k in range(cnt):
+                w_ord[(K, h, k0 + k)] = t[:, k]
+            src = w_tile[(K, h, k0)][:, 0 : cnt * D].bitcast(F32).rearrange("m (k q u) -> m k u q", k=cnt, u=2)
+            order_words(t[:], src, eng)
         def trans_w(K, h, k0, cnt, eng):
             if (K, h) not in w_grp:
                 w_grp[(K, h)] = raw.tile([P, K * D], BF16, name="w_grp%d_%d" % (K, h), align_bytes=64)
@@ -129,7 +143,11 @@ def tile_textheading_pa_t_kernel(tc, words_emb, W2, b2, W3, b3, W4, b4, out):
             for i in range(cnt):
                 words = w_tile[(K, h, k0 + i)][:, 0:D].bitcast(F32)
                 for u in range(2):
-                    nc.tensor.transpose(ps[:, 2 * i + u, :], words[:, u : 256 : 2], ident[:])
+                    if (K, h, k0 + i) in w_ord:
+                        src = w_ord[(K, h, k0 + i)][:, u, :]
+                    else:
+                        src = words[:, u : 256 : 2]
+                    nc.tensor.transpose(ps[:, 2 * i + u, :], src, ident[:])
             src = ps[:, 0 : 2 * cnt, :].rearrange("q (c u) f -> q c f u", u=2)
             if eng == "s":
                 nc.scalar.copy(out=grp_w[:, k0 : k0 + cnt], in_=src)
@@ -150,6 +168,14 @@ def tile_textheading_pa_t_kernel(tc, words_emb, W2, b2, W3, b3, W4, b4, out):
 
         ps_x = {}
         x_grp = {}
+        x_ord = {}
+
+        def order_x(g, half, eng):
+            if half == 0:
+                x_ord[g] = raw.tile([P, NB, 2, P], F32, name="x_ord%d" % g)
+            ns = slice(2 * half, 2 * half + 2)
+            src = x_raw[g][:].rearrange("p n d -> p (n d)").bitcast(F32).rearrange("p (n q u) -> p n u q", n=NB, u=2)
+            order_words(x_ord[g][:, ns], src[:, ns], eng)
 
         def transposes_x(g, halves=(0, 1)):
             banks = ps_x.setdefault(g, [])
@@ -159,7 +185,8 @@ def tile_textheading_pa_t_kernel(tc, words_emb, W2, b2, W3, b3, W4, b4, out):
                 for c in range(2):
                     words = x_raw[g][:, 2 * i + c, :].bitcast(F32)
                     for u in range(2):
-                        nc.tensor.transpose(ps[:, 2 * c + u, :], words[:, u : 256 : 2], perm[:])
+                        src = x_ord[g][:, 2 * i + c, u, :] if g in x_ord else words[:, u : 256 : 2]
+                        nc.tensor.transpose(ps[:, 2 * c + u, :], src, perm[:])
                 banks.append(ps)
 
         def evac_x(g, n, eng):
@@ -347,6 +374,8 @@ def tile_textheading_pa_t_kernel(tc, words_emb, W2, b2, W3, b3, W4, b4, out):
         ps_b = aux.tile([P, P], F32, name="ps_b", tag="aux")
         nc.tensor.transpose(ps_b[:], bias_words[:], ident[:])
         quant_w(3, 0, 2, 1)
+        order_x(1, 0, "v")
+        order_x(1, 1, "v")
         nc.vector.tensor_copy(out=bias_pairs[:], in_=ps_b[:, 0:3])
         quant_w(2, 0, 0, 2)
         nc.vector.tensor_copy(out=bias_sb[:], in_=bias_pairs[:].bitcast(BF16))
@@ -358,11 +387,14 @@ def tile_textheading_pa_t_kernel(tc, words_emb, W2, b2, W3, b3, W4, b4, out):
         quant_x(1)
         passes(0, 0, 2)
         halo(1)
+        order_w(3, 1, 0, 2, "v")
+        order_w(3, 1, 2, 1, "v")
         merge(0, 0, 3)
         trans_w(4, 1, 0, 2, "s")
         trans_w(4, 1, 2, 2, "s")
         merge(0, 0, 2)
         quant_w(4, 1, 0, 4)
+        order_w(2, 1, 0, 2, "v")
         passes(1, 0, 4)
         relu4(1, 0)
         trans_w(3, 1, 0, 2, "s")
@@ -371,11 +403,15 @@ def tile_textheading_pa_t_kernel(tc, words_emb, W2, b2, W3, b3, W4, b4, out):
         quant_w(3, 1, 0, 2)
         passes(1, 0, 3)
         merge(1, 0, 3)
+        order_x(2, 0, "v")
+        order_x(2, 1, "v")
         trans_w(2, 1, 0, 2, "s")
         square(0, 0)
         passes(1, 0, 2)
         quant_w(2, 1, 0, 2)
         merge(1, 0, 2)
+        order_x(3, 0, "v")
+        order_x(3, 1, "v")
         passes(0, 1, 4)
         transposes_x(2)
         relu4(0, 1)
@@ -385,8 +421,12 @@ def tile_textheading_pa_t_kernel(tc, words_emb, W2, b2, W3, b3, W4, b4, out):
         quant_x(2)
         passes(0, 1, 2)
         merge(0, 1, 2)
+        order_x(4, 0, "v")
+        order_x(4, 1, "v")
         halo(2)
         square(1, 0)
+        order_x(5, 0, "s")
+        order_x(5, 1, "s")
         passes(1, 1, 4)
         transposes_x(3)
         relu4(1, 1)
@@ -411,7 +451,9 @@ def tile_textheading_pa_t_kernel(tc, words_emb, W2, b2, W3, b3, W4, b4, out):
                 evac_x(g + 2, 1, "s")
             square(g - 1, 1)
             relu4(g, 0)
-            split_sum(g - 1)
+            add_halves(g - 1, eng="v")
+            high_part(g - 1)
+            low_part(g - 1)
             passes(g, 0, 3)
             merge(g, 0, 3)
             if g + 2 < G:
@@ -428,6 +470,9 @@ def tile_textheading_pa_t_kernel(tc, words_emb, W2, b2, W3, b3, W4, b4, out):
             passes(g, 1, 4)
             relu4(g, 1)
             square(g, 0)
+            if g + 4 < G:
+                order_x(g + 4, 0, "s")
+                order_x(g + 4, 1, "s")
             passes(g, 1, 3)
             merge(g, 1, 3)
             if g + 2 < G:

from contextlib import ExitStack

import concourse.mybir as mybir
from concourse.masks import make_identity

F32 = mybir.dt.float32
BF16 = mybir.dt.bfloat16
U32 = mybir.dt.uint32
I32 = mybir.dt.int32
U8 = mybir.dt.uint8
FP8X4 = mybir.dt.float8_e4m3fn_x4
ACT = mybir.ActivationFunctionType
ALU = mybir.AluOpType

P = 128
B, T, D, F = 32, 128, 512, 256
WIDTHS = (4, 3, 2)
NB = 4
G = B // NB
LAST = G - 1
BLK = 64
UNIT0 = {4: 0, 3: 4, 2: 7}
BIAS_COL = {4: 0, 3: 2, 2: 4}
NCOL = 1024
FLOPS = 2 * B * D * F * (2 * 127 + 3 * 126 + 4 * 125)
WARM = 4


def tile_textheading_pa_t_kernel(tc, words_emb, W2, b2, W3, b3, W4, b4, out):
    nc = tc.nc
    w_dram = {2: W2, 3: W3, 4: W4}
    b_dram = {2: b2, 3: b3, 4: b4}
    with ExitStack() as ctx:
        const = ctx.enter_context(tc.tile_pool(name="const", bufs=1))
        raw = ctx.enter_context(tc.tile_pool(name="raw", bufs=1))
        xg = ctx.enter_context(tc.tile_pool(name="xg", bufs=3))
        code_pool = ctx.enter_context(tc.tile_pool(name="code", bufs=5))
        work = ctx.enter_context(tc.tile_pool(name="work", bufs=3))
        split = ctx.enter_context(tc.tile_pool(name="split", bufs=3))
        outp = ctx.enter_context(tc.tile_pool(name="outp", bufs=3))
        mxp = ctx.enter_context(tc.psum_pool(name="mxp", bufs=5))
        aux = ctx.enter_context(tc.psum_pool(name="aux", bufs=3))
        ctx.enter_context(tc.manual_schedule())

        bias_words = const.tile([P, P], F32, name="bias_words")
        nc.vector.memset(bias_words[:], 0.0)
        for K in WIDTHS:
            row = BIAS_COL[K] // 2
            nc.scalar.dma_start(
                out=bias_words[row : row + 1, :], in_=b_dram[K].bitcast(F32).rearrange("(o m) -> o m", o=1)
            )
        x_raw = {}
        w_tile = {}

        def load_x(g, pieces=1):
            t = raw.tile([P, NB, D], BF16, name="x_raw%d" % g)
            src = words_emb[g * NB : (g + 1) * NB].rearrange("n p d -> p n d")
            step = NB // pieces
            for n in range(0, NB, step):
                nc.sync.dma_start(out=t[:, n : n + step, :], in_=src[:, n : n + step, :])
            x_raw[g] = t

        def load_w(K, h, k0, cnt):
            t = raw.tile([P, cnt * D], BF16, name="w_raw%d_%d_%d" % (K, h, k0))
            src = w_dram[K].rearrange("(m h) k d -> h m k d", h=2)[h]
            nc.sync.dma_start(
                out=t[:].rearrange("m (k d) -> m k d", k=cnt), in_=src[:, k0 : k0 + cnt, :]
            )
            for k in range(cnt):
                w_tile[(K, h, k0 + k)] = t[:, k * D : cnt * D]

        load_x(0, pieces=2)
        load_w(4, 0, 0, 2)
        load_w(4, 0, 2, 2)
        load_w(3, 0, 0, 3)
        load_w(2, 0, 0, 2)
        load_x(1)
        load_w(4, 1, 0, 4)
        load_w(3, 1, 0, 3)
        load_w(2, 1, 0, 2)
        for g in range(2, G):
            load_x(g)

        warm = const.tile([P, 512], BF16, name="warm")
        nc.vector.memset(warm[:], 0.0)
        one_col = const.tile([P, 1], F32, name="one_col")
        nc.vector.memset(one_col[:], 1.0)
        dummy = const.tile([P, 1], F32, name="dummy")
        nc.scalar.activation(out=dummy[:], in_=one_col[:], func=ACT.Abs_reciprocal_sqrt)
        ident = const.tile([P, P], F32, name="ident")
        make_identity(nc, ident[:])
        perms = {}
        for L in (8, 4):
            perms[L] = const.tile([P, P], F32, name="perm%d" % L)
            nc.vector.tensor_copy(
                out=perms[L][:].rearrange("i (pl ph) -> i pl ph", pl=L),
                in_=ident[:].rearrange("i (ph pl) -> i pl ph", pl=L),
            )
        zeros = const.tile([P, NB * 3], F32, name="zeros")
        nc.vector.memset(zeros[:], 0.0)
        ones_bf = const.tile([P, P], BF16, name="ones_bf")
        nc.vector.memset(ones_bf[:], 1.0)
        ones_f32 = const.tile([P, P], F32, name="ones_f32")
        nc.vector.memset(ones_f32[:], 1.0)
        planes = []
        for i in range(3):
            c = const.tile([P, NCOL], U32, name="x_codes%d" % i, align_bytes=64)
            s = const.tile([P, NCOL], U8, name="x_scales%d" % i, align_bytes=64)
            nc.gpsimd.memset(s[:].bitcast(U32), 0)
            planes.append((c, s))

        w_codes = const.tile([P, 18 * P], U32, name="w_codes", align_bytes=64)
        w_scales = const.tile([P, 18 * P], U8, name="w_scales", align_bytes=64)
        bias_sb = const.tile([P, 6], F32, name="bias_sb")
        bias_pairs = const.tile([P, 3], F32, name="bias_pairs")

        ps_warm = aux.tile([P, 512], F32, name="ps_warm", tag="aux")

        def warm_up(count):
            for i in range(count):
                nc.tensor.matmul(out=ps_warm[:], lhsT=warm[:, 0:P], rhs=warm[:], start=True, stop=True)

        w_grp = {}
        w_ord = {}

        def order_words(out, src, eng):
            if eng == "s":
                nc.scalar.copy(out=out, in_=src)
            else:
                nc.vector.tensor_copy(out=out, in_=src)

        def order_w(K, h, k0, cnt, eng):
            t = raw.tile([P, cnt, 2, P], F32, name="w_ord%d_%d_%d" % (K, h, k0))
            for k in range(cnt):
                w_ord[(K, h, k0 + k)] = t[:, k]
            src = w_tile[(K, h, k0)][:, 0 : cnt * D].bitcast(F32).rearrange("m (k q u) -> m k u q", k=cnt, u=2)
            order_words(t[:], src, eng)
        def trans_w(K, h, k0, cnt, eng):
            if (K, h) not in w_grp:
                w_grp[(K, h)] = raw.tile([P, K * D], BF16, name="w_grp%d_%d" % (K, h), align_bytes=64)
            grp_w = w_grp[(K, h)][:].bitcast(F32).rearrange("q (c f u) -> q c f u", c=K, f=P, u=2)
            ps = mxp.tile([P, 4, P], F32, name="ps_w", tag="acc")
            for i in range(cnt):
                words = w_tile[(K, h, k0 + i)][:, 0:D].bitcast(F32)
                for u in range(2):
                    if (K, h, k0 + i) in w_ord:
                        src = w_ord[(K, h, k0 + i)][:, u, :]
                    else:
                        src = words[:, u : 256 : 2]
                    nc.tensor.transpose(ps[:, 2 * i + u, :], src, ident[:])
            src = ps[:, 0 : 2 * cnt, :].rearrange("q (c u) f -> q c f u", u=2)
            if eng == "s":
                nc.scalar.copy(out=grp_w[:, k0 : k0 + cnt], in_=src)
            else:
                nc.vector.tensor_copy(out=grp_w[:, k0 : k0 + cnt], in_=src)

        def quant_w(K, h, k0, cnt):
            unit = h * 9 + UNIT0[K]
            cols = slice((unit + k0) * P, (unit + k0 + cnt) * P)
            nc.vector.quantize_mx(
                out=w_codes[:, cols].bitcast(FP8X4),
                scales=w_scales[:, cols],
                in_=w_grp[(K, h)][:, k0 * D : (k0 + cnt) * D],
            )

        def parts(g):
            return ((g * NB, NB, 0, 8),)

        ps_x = {}
        x_grp = {}
        x_ord = {}

        def order_x(g, half, eng):
            if half == 0:
                x_ord[g] = raw.tile([P, NB, 2, P], F32, name="x_ord%d" % g)
            ns = slice(2 * half, 2 * half + 2)
            src = x_raw[g][:].rearrange("p n d -> p (n d)").bitcast(F32).rearrange("p (n q u) -> p n u q", n=NB, u=2)
            order_words(x_ord[g][:, ns], src[:, ns], eng)

        def transposes_x(g, halves=(0, 1)):
            banks = ps_x.setdefault(g, [])
            perm = perms[parts(g)[0][3]]
            for i in halves:
                ps = aux.tile([P, 4, P], F32, name="ps_x", tag="aux")
                for c in range(2):
                    words = x_raw[g][:, 2 * i + c, :].bitcast(F32)
                    for u in range(2):
                        src = x_ord[g][:, 2 * i + c, u, :] if g in x_ord else words[:, u : 256 : 2]
                        nc.tensor.transpose(ps[:, 2 * c + u, :], src, perm[:])
                banks.append(ps)

        def evac_x(g, n, eng):
            if g not in x_grp:
                x_grp[g] = xg.tile([P, 512 * 4], BF16, name="x_grp", align_bytes=64)
            n0, nb, c0, L = parts(g)[n * len(parts(g)) // NB]
            grp = x_grp[g][:, c0 * 2 : c0 * 2 + L * BLK * 4].bitcast(F32)
            dst = grp.rearrange("q (l n ph u) -> q l n ph u", l=L, n=nb, u=2)[:, :, n % nb]
            src = ps_x[g][n // 2][:, 2 * (n % 2) : 2 * (n % 2) + 2, :].rearrange("q u (l ph) -> q l ph u", l=L)
            if eng == "v":
                nc.vector.tensor_copy(out=dst, in_=src)
            else:
                nc.scalar.copy(out=dst, in_=src)

        def quant_x(g):
            codes, scales = planes[g % 3]
            for n0, nb, c0, L in parts(g):
                w = L * BLK
                nc.vector.quantize_mx(
                    out=codes[:, c0 : c0 + w].bitcast(FP8X4),
                    scales=scales[:, c0 : c0 + w],
                    in_=x_grp[g][:, c0 * 2 : c0 * 2 + w * 4],
                )

        def halo(g):
            codes, scales = planes[g % 3]
            r = 3 * BLK
            for n0, nb, c0, L in parts(g):
                w = c0 + L * BLK
                nc.vector.tensor_copy(
                    out=codes[:, w : w + r].bitcast(I32), in_=codes[:, c0 + 1 : c0 + 1 + r].bitcast(I32)
                )
                nc.vector.tensor_copy(out=scales[:, w : w + r], in_=scales[:, c0 + 1 : c0 + 1 + r])

        accs = {}
        code_of = {}

        def passes(g, h, K, s=0):
            n0, nb, c0, L = parts(g)[s]
            codes, scales = planes[g % 3]
            acc = mxp.tile([P, L * BLK], F32, name="acc", tag="acc")
            for k in range(K):
                unit = h * 9 + UNIT0[K] + k
                cols = slice(c0 + k * BLK, c0 + (k + L) * BLK)
                nc.tensor.matmul_mx(
                    out=acc[:],
                    lhsT=w_codes[:, unit * P : (unit + 1) * P].bitcast(FP8X4),
                    lhsT_scale=w_scales[:, unit * P : (unit + 1) * P],
                    rhs=codes[:, cols].bitcast(FP8X4),
                    rhs_scale=scales[:, cols],
                    start=(k == 0),
                    stop=(k == K - 1),
                )
            accs[(g, h, K, s)] = acc

        def relu4(g, h, s=0):
            n0, nb, c0, L = parts(g)[s]
            code = code_pool.tile([P, nb * T], F32, name="code%d" % h)
            code_of[(g, h, s)] = code
            nc.scalar.activation(
                out=code[:].rearrange("f (m a b) -> f a m b", a=L // 4, b=4),
                in_=accs[(g, h, 4, s)][:].rearrange("f (a b m) -> f a m b", a=L // 4, b=4),
                func=ACT.Relu,
                bias=bias_sb[:, BIAS_COL[4] + h : BIAS_COL[4] + h + 1],
            )
            nc.scalar.copy(
                out=code[:].rearrange("f (n p) -> f n p", p=T)[:, :, T - 3 : T],
                in_=zeros[:, 0 : nb * 3].rearrange("f (n p) -> f n p", p=3),
            )

        def merge(g, h, K, ns=slice(0, NB), s=0):
            n0, nb, c0, L = parts(g)[s]
            ms = slice(ns.start * T // L, ns.stop * T // L)
            code_v = code_of[(g, h, s)][:].rearrange("f (m l) -> f m l", l=L)
            acc_v = accs[(g, h, K, s)][:].rearrange("f (l m) -> f m l", l=L)
            for a in range(0, L, 4):
                nc.vector.scalar_tensor_tensor(
                    out=code_v[:, ms, a : a + 4],
                    in0=acc_v[:, ms, a : a + 4],
                    scalar=bias_sb[:, BIAS_COL[K] + h : BIAS_COL[K] + h + 1],
                    in1=code_v[:, ms, a : a + 4],
                    op0=ALU.add,
                    op1=ALU.max,
                )

        sqs = {}
        his = {}
        los = {}
        rinvs = {}
        sss = {}
        outs = {}

        def width(g, s):
            return parts(g)[s][1] * T

        def square(g, h, ns=slice(0, NB), s=0):
            n0, nb, c0, L = parts(g)[s]
            nc.scalar.activation(
                out=code_of[(g, h, s)][:].rearrange("f (n p) -> f n p", p=T)[:, ns, T - 2],
                in_=accs[(g, h, 2, s)][:].rearrange("f (l n ph) -> f l n ph", l=L, n=nb)[:, L - 2, ns, T // L - 1],
                func=ACT.Relu,
                bias=bias_sb[:, BIAS_COL[2] + h : BIAS_COL[2] + h + 1],
            )
            if (g, h, s) not in sqs:
                sqs[(g, h, s)] = work.tile([P, width(g, s)], F32, name="sq%d" % h)
            cs = slice(ns.start * T, ns.stop * T)
            nc.scalar.activation(out=sqs[(g, h, s)][:, cs], in_=code_of[(g, h, s)][:, cs], func=ACT.Square)

        tots = {}

        def add_halves(g, s=0, eng="p"):
            tots[(g, s)] = work.tile([P, width(g, s)], F32, name="tot")
            e = nc.gpsimd if eng == "p" else nc.vector
            e.tensor_tensor(out=tots[(g, s)][:], in0=sqs[(g, 0, s)][:], in1=sqs[(g, 1, s)][:], op=ALU.add)

        def high_part(g, s=0, eng="p"):
            his[(g, s)] = split.tile([P, width(g, s)], BF16, name="hi")
            if eng == "p":
                nc.gpsimd.tensor_scalar(
                    out=his[(g, s)][:], in0=tots[(g, s)][:], scalar1=1.0, scalar2=0.0, op0=ALU.mult, op1=ALU.add
                )
            else:
                nc.scalar.copy(out=his[(g, s)][:], in_=tots[(g, s)][:])

        def low_part(g, s=0, eng="p"):
            los[(g, s)] = split.tile([P, width(g, s)], BF16, name="lo")
            e = nc.gpsimd if eng == "p" else nc.vector
            e.tensor_tensor(out=los[(g, s)][:], in0=tots[(g, s)][:], in1=his[(g, s)][:], op=ALU.subtract)

        def split_sum(g, s=0):
            add_halves(g, s)
            high_part(g, s)
            low_part(g, s)

        def sum_filters(g, s=0):
            ss = aux.tile([P, width(g, s)], F32, name="ss", tag="aux")
            nc.tensor.matmul(out=ss[:], lhsT=ones_bf[:], rhs=his[(g, s)][:], start=True, stop=False)
            nc.tensor.matmul(out=ss[:], lhsT=ones_bf[:], rhs=los[(g, s)][:], start=False, stop=True)
            sss[(g, s)] = ss

        def rsqrt(g, s=0):
            rinvs[(g, s)] = work.tile([P, width(g, s)], F32, name="rinv")
            nc.scalar.activation(out=rinvs[(g, s)][:], in_=sss[(g, s)][:], func=ACT.Abs_reciprocal_sqrt)

        def scale(g, h, s=0):
            n0, nb, c0, L = parts(g)[s]
            if h == 0:
                outs[(g, s)] = outp.tile([P, nb, 2, T - 1], F32, name="o")
            nc.vector.scalar_tensor_tensor(
                out=outs[(g, s)][:, :, h, :],
                in0=rinvs[(g, s)][:].rearrange("f (n p) -> f n p", p=T)[:, :, 0 : T - 1],
                scalar=1.0e12,
                in1=code_of[(g, h, s)][:].rearrange("f (n p) -> f n p", p=T)[:, :, 0 : T - 1],
                op0=ALU.min,
                op1=ALU.mult,
            )
            if h == 1:
                nc.sync.dma_start(
                    out=out[n0 : n0 + nb].rearrange("n (m h) p -> m n (h p)", h=2),
                    in_=outs[(g, s)][:].rearrange("m n h p -> m n (h p)"),
                )

        def evac4(g, engines):
            for n in range(NB):
                evac_x(g, n, engines[n])

        warm_up(WARM)
        transposes_x(0, (0,))
        evac_x(0, 0, "s")
        evac_x(0, 1, "v")
        transposes_x(0, (1,))
        evac_x(0, 2, "s")
        evac_x(0, 3, "v")
        trans_w(4, 0, 0, 2, "s")
        quant_x(0)
        trans_w(4, 0, 2, 2, "s")
        warm_up(2)
        quant_w(4, 0, 0, 2)
        halo(0)
        quant_w(4, 0, 2, 2)
        trans_w(3, 0, 0, 2, "s")
        trans_w(3, 0, 2, 1, "v")
        quant_w(3, 0, 0, 2)
        trans_w(2, 0, 0, 2, "s")
        ps_b = aux.tile([P, P], F32, name="ps_b", tag="aux")
        nc.tensor.transpose(ps_b[:], bias_words[:], ident[:])
        quant_w(3, 0, 2, 1)
        order_x(1, 0, "v")
        order_x(1, 1, "v")
        nc.vector.tensor_copy(out=bias_pairs[:], in_=ps_b[:, 0:3])
        quant_w(2, 0, 0, 2)
        nc.vector.tensor_copy(out=bias_sb[:], in_=bias_pairs[:].bitcast(BF16))
        passes(0, 0, 4)
        relu4(0, 0)
        transposes_x(1)
        evac4(1, "vvvs")
        passes(0, 0, 3)
        quant_x(1)
        passes(0, 0, 2)
        halo(1)
        order_w(3, 1, 0, 2, "v")
        order_w(3, 1, 2, 1, "v")
        merge(0, 0, 3)
        trans_w(4, 1, 0, 2, "s")
        trans_w(4, 1, 2, 2, "s")
        merge(0, 0, 2)
        quant_w(4, 1, 0, 4)
        order_w(2, 1, 0, 2, "v")
        passes(1, 0, 4)
        relu4(1, 0)
        trans_w(3, 1, 0, 2, "s")
        trans_w(3, 1, 2, 1, "v")
        quant_w(3, 1, 2, 1)
        quant_w(3, 1, 0, 2)
        passes(1, 0, 3)
        merge(1, 0, 3)
        order_x(2, 0, "v")
        order_x(2, 1, "v")
        trans_w(2, 1, 0, 2, "s")
        square(0, 0)
        passes(1, 0, 2)
        quant_w(2, 1, 0, 2)
        merge(1, 0, 2)
        order_x(3, 0, "v")
        order_x(3, 1, "v")
        passes(0, 1, 4)
        transposes_x(2)
        relu4(0, 1)
        evac4(2, "svsv")
        passes(0, 1, 3)
        merge(0, 1, 3)
        quant_x(2)
        passes(0, 1, 2)
        merge(0, 1, 2)
        order_x(4, 0, "v")
        order_x(4, 1, "v")
        halo(2)
        square(1, 0)
        order_x(5, 0, "s")
        order_x(5, 1, "s")
        passes(1, 1, 4)
        transposes_x(3)
        relu4(1, 1)
        square(0, 1)
        split_sum(0)
        passes(1, 1, 3)
        evac4(3, "svsv")
        merge(1, 1, 3)
        passes(1, 1, 2)
        merge(1, 1, 2)
        quant_x(3)
        transposes_x(4)

        for g in range(2, LAST):
            passes(g, 0, 4)
            halo(g + 1)
            if g > 2:
                rsqrt(g - 2)
                scale(g - 2, 0)
                scale(g - 2, 1)
            if g + 2 < G:
                evac_x(g + 2, 1, "s")
            square(g - 1, 1)
            relu4(g, 0)
            add_halves(g - 1, eng="v")
            high_part(g - 1)
            low_part(g - 1)
            passes(g, 0, 3)
            merge(g, 0, 3)
            if g + 2 < G:
                evac_x(g + 2, 0, "v")
                evac_x(g + 2, 2, "s")
                evac_x(g + 2, 3, "s")
            passes(g, 0, 2)
            merge(g, 0, 2)
            if g == 2:
                sum_filters(0)
                rsqrt(0)
                scale(0, 0)
                scale(0, 1)
            passes(g, 1, 4)
            relu4(g, 1)
            square(g, 0)
            if g + 4 < G:
                order_x(g + 4, 0, "s")
                order_x(g + 4, 1, "s")
            passes(g, 1, 3)
            merge(g, 1, 3)
            if g + 2 < G:
                quant_x(g + 2)
            passes(g, 1, 2)
            merge(g, 1, 2)
            if g + 3 < G:
                transposes_x(g + 3)
            sum_filters(g - 1)

        g = LAST
        halves = (slice(0, 2), slice(2, 4))
        passes(g, 0, 4)
        square(g - 1, 1)
        rsqrt(g - 2)
        relu4(g, 0)
        scale(g - 2, 0)
        scale(g - 2, 1)
        split_sum(g - 1)
        passes(g, 0, 3)
        merge(g, 0, 3)
        passes(g, 0, 2)
        merge(g, 0, 2)
        passes(g, 1, 4)
        relu4(g, 1)
        square(g, 0)
        passes(g, 1, 3)
        merge(g, 1, 3)
        passes(g, 1, 2)
        sum_filters(g - 1)
        last_ss = []
        for ns in halves:
            ss = aux.tile([P, 2 * T], F32, name="ss_last", tag="aux")
            cs = slice(ns.start * T, ns.stop * T)
            nc.tensor.matmul(out=ss[:], lhsT=ones_f32[:], rhs=sqs[(g, 0, 0)][:, cs], start=True, stop=False)
            last_ss.append(ss)
        merge(g, 1, 2, halves[0])
        square(g, 1, halves[0])
        rsqrt(g - 1)
        merge(g, 1, 2, halves[1])
        square(g, 1, halves[1])
        scale(g - 1, 0)
        scale(g - 1, 1)
        rinv = work.tile([P, NB * T], F32, name="rinv")
        for i, ns in enumerate(halves):
            cs = slice(ns.start * T, ns.stop * T)
            nc.tensor.matmul(out=last_ss[i][:], lhsT=ones_f32[:], rhs=sqs[(g, 1, 0)][:, cs], start=False, stop=True)
            nc.scalar.activation(out=rinv[:, cs], in_=last_ss[i][:], func=ACT.Abs_reciprocal_sqrt)
        for i, ns in enumerate(halves):
            cs = slice(ns.start * T, ns.stop * T)
            o = outp.tile([P, NB // 2, 2, T - 1], F32, name="o_last")
            for h in range(2):
                nc.vector.scalar_tensor_tensor(
                    out=o[:, :, h, :],
                    in0=rinv[:, cs].rearrange("f (n p) -> f n p", p=T)[:, :, 0 : T - 1],
                    scalar=1.0e12,
                    in1=code_of[(g, h, 0)][:, cs].rearrange("f (n p) -> f n p", p=T)[:, :, 0 : T - 1],
                    op0=ALU.min,
                    op1=ALU.mult,
                )
            n0 = g * NB + 2 * i
            queue = nc.sync if i == 0 else nc.scalar
            queue.dma_start(
                out=out[n0 : n0 + 2].rearrange("n (m h) p -> m n (h p)", h=2),
                in_=o[:].rearrange("m n h p -> m n (h p)"),
            )
